import numpy as np
import ml_dtypes


def mxq(x, axis, fmt="e4m3"):
    dtype, down = {"e4m3": (ml_dtypes.float8_e4m3fn, 7), "e5m2": (ml_dtypes.float8_e5m2, 14)}[fmt]
    v = np.moveaxis(np.asarray(x, np.float32).astype(ml_dtypes.bfloat16).astype(np.float64), axis, -1)
    blocks = v.reshape(v.shape[:-1] + (-1, 32))
    amax = np.abs(blocks).max(-1, keepdims=True)
    byte = np.maximum(np.where(amax > 0, np.frexp(amax)[1] - 1 + 127, 0) - down, 1)
    scale = np.exp2(byte - 127.0)
    codes = (blocks / scale).astype(np.float32).astype(dtype).astype(np.float64)
    return np.moveaxis((codes * scale).reshape(v.shape), -1, axis)


WIDE = False


def mx_kscale(k):
    if not WIDE:
        return np.ones(k)
    levels = np.array([10, -10, 5, -5, 0])
    if k % 512:
        return np.exp2(np.random.permutation(np.resize(levels, k // 32))).repeat(32)
    a = np.empty((k // 512, 16))
    for p in range(k // 512):
        a[p, :8] = np.random.permutation(np.resize(levels, 8))
        for g in range(8):
            far = levels[np.abs(levels - a[p, g]) >= 10]
            a[p, g + 8] = far[np.random.randint(len(far))]
    return np.exp2(a.ravel()).repeat(32)


BF16 = ml_dtypes.bfloat16


def bf(x):
    return np.asarray(x, np.float32).astype(BF16)


def f64(x):
    return np.asarray(x).astype(np.float64)


B, S, D, H, QL, KVL, RD, ND, VD = 2, 2048, 1024, 4, 512, 512, 64, 64, 128
QHD = ND + RD
ROPE_THETA, ROPE_RATIO = 10000.0, 1.0


def rope_tables(seq_len):
    half = RD // 2
    inv_freq = ROPE_RATIO / (ROPE_THETA ** (np.arange(half) * 2.0 / RD))
    freqs = np.arange(seq_len)[:, None] * inv_freq[None, :]
    return np.cos(freqs), np.sin(freqs)


def apply_rope(x, cos, sin):
    x_even = x[..., 0::2]
    x_odd = x[..., 1::2]
    r_even = x_even * cos - x_odd * sin
    r_odd = x_odd * cos + x_even * sin
    return np.stack([r_even, r_odd], axis=-1).reshape(x.shape)


def setup_inputs():
    s, t = mx_kscale(D), mx_kscale(QL)
    return {"hidden_states": bf(np.random.standard_normal((B, S, D)) * s),
            "Wqa": bf(np.random.standard_normal((D, QL)) / np.sqrt(D) / s[:, None] * t),
            "Wqb": bf(np.random.standard_normal((QL, H * QHD)) / np.sqrt(QL) / t[:, None])}


def reference(hidden_states, Wqa, Wqb):
    q_latent = mxq(f64(hidden_states), 2, "e4m3") @ mxq(f64(Wqa), 0, "e4m3")
    q = (mxq(q_latent, 2, "e4m3") @ mxq(f64(Wqb), 0, "e4m3")).reshape(B, S, H, QHD)
    q = q.transpose(0, 2, 1, 3)
    q_nope, q_pe = q[..., :ND], q[..., ND:]
    cos, sin = rope_tables(S)
    q_pe = apply_rope(q_pe, cos, sin)
    return np.concatenate([q_nope, q_pe], axis=-1)

@@ -1,0 +1,294 @@
+import math
+from contextlib import ExitStack
+
+import concourse.mybir as mybir
+from concourse.masks import make_identity
+
+F32 = mybir.dt.float32
+BF16 = mybir.dt.bfloat16
+I32 = mybir.dt.int32
+U32 = mybir.dt.uint32
+U8 = mybir.dt.uint8
+FP8X4 = mybir.dt.float8_e4m3fn_x4
+ALU = mybir.AluOpType
+FUNC = mybir.ActivationFunctionType
+
+P = 128
+PACK = 4
+BATCH, SEQ, D_MODEL, Q_LATENT = 2, 2048, 1024, 512
+HEADS, HEAD_DIM, NOPE_DIM = 4, 128, 64
+ROPE_DIM = HEAD_DIM - NOPE_DIM
+PAIRS = ROPE_DIM // 2
+ROPE_THETA = 10000.0
+
+K_PASS = P * PACK
+PASSES_A = D_MODEL // K_PASS
+WORDS = D_MODEL // 2
+LATENT_BLOCKS = Q_LATENT // P
+TILES_PER_BATCH = SEQ // P
+N_TILES = BATCH * TILES_PER_BATCH
+LOAD_TILES = 2
+STORE_TILES = 2
+RUN_TILES = 2
+LEAD_TILES = 3
+
+FLOPS = 2 * BATCH * SEQ * (D_MODEL * Q_LATENT + Q_LATENT * HEADS * HEAD_DIM)
+
+
+def tile_mlaattention_pa_t_kernel(tc, hidden_states, Wqa, Wqb, out):
+    nc = tc.nc
+    with ExitStack() as ctx:
+        ctx.enter_context(tc.manual_schedule())
+        const = ctx.enter_context(tc.tile_pool(name="const", bufs=1))
+        x_pool = ctx.enter_context(tc.tile_pool(name="x", bufs=N_TILES // LOAD_TILES))
+        xg_pool = ctx.enter_context(tc.tile_pool(name="xg", bufs=4))
+        xq_pool = ctx.enter_context(tc.tile_pool(name="xq", bufs=LEAD_TILES + 2))
+        lat_pool = ctx.enter_context(tc.tile_pool(name="lat", bufs=3))
+        rope_pool = ctx.enter_context(tc.tile_pool(name="rope", bufs=2))
+        out_pool = ctx.enter_context(tc.tile_pool(name="outp", bufs=4))
+        xt_psum = ctx.enter_context(tc.psum_pool(name="xt_psum", bufs=3))
+        lat_psum = ctx.enter_context(tc.psum_pool(name="lat_psum", bufs=2))
+        q_psum = ctx.enter_context(tc.psum_pool(name="q_psum", bufs=3))
+
+        wa_raw = const.tile([P, PASSES_A, PACK, Q_LATENT], BF16)
+        for c in range(PASSES_A):
+            nc.sync.dma_start(
+                out=wa_raw[:, c],
+                in_=Wqa[c * K_PASS : (c + 1) * K_PASS, :].rearrange("(p j) n -> p j n", j=PACK),
+            )
+        wb_raw = const.tile([P, PACK, Q_LATENT], BF16)
+        x_tiles = []
+        for g in range(N_TILES // LOAD_TILES):
+            b, t0 = divmod(g * LOAD_TILES, TILES_PER_BATCH)
+            x_sb = x_pool.tile([P, LOAD_TILES, D_MODEL], BF16)
+            nc.sync.dma_start(
+                out=x_sb[:],
+                in_=hidden_states[b].rearrange("(r t) k -> r t k", t=TILES_PER_BATCH)[:, t0 : t0 + LOAD_TILES, :],
+            )
+            x_tiles.append(x_sb)
+            if g == 1:
+                nc.sync.dma_start(out=wb_raw[:], in_=Wqb.rearrange("(p j) n -> p j n", j=PACK))
+
+        ident = const.tile([P, P], F32)
+        make_identity(nc, ident[:])
+        pos_i = const.tile([P, TILES_PER_BATCH], I32)
+        nc.gpsimd.iota(pos_i[:], pattern=[[1, TILES_PER_BATCH]], base=0, channel_multiplier=TILES_PER_BATCH)
+
+        warm = const.tile([P, 2], F32)
+        nc.vector.memset(warm[:], 0.0)
+        nc.scalar.activation(out=warm[:, 1:2], in_=warm[:, 0:1], func=FUNC.Sin)
+
+        pos_f = const.tile([P, TILES_PER_BATCH], F32)
+        nc.vector.tensor_copy(out=pos_f[:], in_=pos_i[:])
+        turns = const.tile([P, PAIRS, TILES_PER_BATCH], F32)
+        for i in range(PAIRS):
+            nc.vector.tensor_scalar_mul(
+                out=turns[:, i, :], in0=pos_f[:], scalar1=ROPE_THETA ** (-2.0 * i / ROPE_DIM) / (2.0 * math.pi)
+            )
+        turns_flat = turns[:].rearrange("p i t -> p (i t)")
+        whole_i = const.tile([P, PAIRS * TILES_PER_BATCH], I32)
+        nc.vector.tensor_copy(out=whole_i[:], in_=turns_flat)
+        whole_f = const.tile([P, PAIRS * TILES_PER_BATCH], F32)
+        nc.vector.tensor_copy(out=whole_f[:], in_=whole_i[:])
+        left = const.tile([P, PAIRS * TILES_PER_BATCH], F32)
+        nc.vector.tensor_tensor(out=left[:], in0=turns_flat, in1=whole_f[:], op=ALU.subtract)
+        minus = const.tile([P, PAIRS, TILES_PER_BATCH], F32)
+        minus_flat = minus[:].rearrange("p i t -> p (i t)")
+        nc.vector.scalar_tensor_tensor(
+            out=minus_flat, in0=left[:], scalar=0.5, in1=left[:], op0=ALU.is_gt, op1=ALU.subtract
+        )
+        sin_pm = const.tile([P, TILES_PER_BATCH, 2, PAIRS], F32)
+        minus_ti = minus[:].rearrange("p i t -> p t i")
+        nc.scalar.activation(out=sin_pm[:, :, 0, :], in_=minus_ti, func=FUNC.Sin, scale=2.0 * math.pi)
+        nc.scalar.activation(out=sin_pm[:, :, 1, :], in_=minus_ti, func=FUNC.Sin, scale=-2.0 * math.pi)
+        half_sin = const.tile([P, PAIRS * TILES_PER_BATCH], F32)
+        nc.scalar.activation(out=half_sin[:], in_=minus_flat, func=FUNC.Sin, scale=math.pi)
+        twice_sq = const.tile([P, PAIRS, TILES_PER_BATCH], F32)
+        nc.scalar.activation(
+            out=twice_sq[:].rearrange("p i t -> p (i t)"), in_=half_sin[:], func=FUNC.Square, scale=math.sqrt(2.0)
+        )
+        cos2 = const.tile([P, TILES_PER_BATCH, PAIRS, 2], F32)
+
+        wa_grouped = const.tile([P, PASSES_A, Q_LATENT, PACK], BF16, align_bytes=64)
+        wa_codes = const.tile([P, PASSES_A, Q_LATENT], U32, align_bytes=64)
+        wa_scales = const.tile([P, PASSES_A, Q_LATENT], U8, align_bytes=64)
+        for c in range(PASSES_A):
+            nc.vector.tensor_copy(
+                out=wa_grouped[:, c].rearrange("p (m q) t -> p m q t", m=LATENT_BLOCKS),
+                in_=wa_raw[:, c].rearrange("p t (q m) -> p m q t", m=LATENT_BLOCKS),
+            )
+        for c in range(PASSES_A):
+            nc.vector.quantize_mx(
+                out=wa_codes[:, c, :].bitcast(FP8X4),
+                scales=wa_scales[:, c, :],
+                in_=wa_grouped[:, c].rearrange("p n t -> p (n t)"),
+            )
+        wb_grouped = const.tile([P, Q_LATENT, PACK], BF16, align_bytes=64)
+        wb_codes = const.tile([P, Q_LATENT], U32, align_bytes=64)
+        wb_scales = const.tile([P, Q_LATENT], U8, align_bytes=64)
+
+        def prepare_wqb_and_cos():
+            nc.vector.tensor_copy(out=wb_grouped[:], in_=wb_raw[:].rearrange("p j n -> p n j"))
+            nc.vector.tensor_scalar(
+                out=cos2[:],
+                in0=twice_sq[:].rearrange("p i t -> p t i").unsqueeze(3).to_broadcast([P, TILES_PER_BATCH, PAIRS, 2]),
+                scalar1=-1.0,
+                scalar2=1.0,
+                op0=ALU.mult,
+                op1=ALU.add,
+            )
+            nc.vector.quantize_mx(
+                out=wb_codes[:].bitcast(FP8X4), scales=wb_scales[:], in_=wb_grouped[:].rearrange("p n j -> p (n j)")
+            )
+
+        xt_banks, xg_tiles, xq_tiles = {}, {}, {}
+        lat_banks, lat_tiles, latq_tiles = {}, {}, {}
+        q_banks, rope_tiles, out_tiles = {}, {}, {}
+
+        def transpose_x(n):
+            words = x_tiles[n // LOAD_TILES][:, n % LOAD_TILES, :].bitcast(F32)
+            xt = xt_psum.tile([P, WORDS // P, P], F32)
+            for w in range(WORDS // P):
+                first = 2 * P * (w // 2) + w % 2
+                nc.tensor.transpose(xt[:, w, :], words[:, first : 2 * P * (w // 2 + 1) : 2], ident[:])
+            xt_banks[n] = xt
+
+        def copy_x(n):
+            xg = xg_pool.tile([P, PASSES_A, P, PACK], BF16, align_bytes=64)
+            nc.scalar.copy(
+                out=xg[:].rearrange("p c r t -> p c (r t)").bitcast(F32).rearrange("p c (r u) -> p c r u", u=2),
+                in_=xt_banks[n][:].rearrange("p (c u) r -> p c r u", u=2),
+            )
+            xg_tiles[n] = xg
+
+        def quantise_x(n):
+            x_codes = xq_pool.tile([P, PASSES_A, P], U32, align_bytes=64)
+            x_scales = xq_pool.tile([P, PASSES_A, P], U8, align_bytes=64)
+            nc.vector.quantize_mx(
+                out=x_codes[:].rearrange("p c r -> p (c r)").bitcast(FP8X4),
+                scales=x_scales[:].rearrange("p c r -> p (c r)"),
+                in_=xg_tiles[n][:].rearrange("p c r t -> p (c r t)"),
+            )
+            xq_tiles[n] = (x_codes, x_scales)
+
+        def first_matmul(n):
+            x_codes, x_scales = xq_tiles[n]
+            lat_ps = lat_psum.tile([P, LATENT_BLOCKS, P], F32)
+            for m in range(LATENT_BLOCKS):
+                for c in range(PASSES_A):
+                    nc.tensor.matmul_mx(
+                        out=lat_ps[:, m, :],
+                        lhsT=wa_codes[:, c, m * P : (m + 1) * P].bitcast(FP8X4),
+                        lhsT_scale=wa_scales[:, c, m * P : (m + 1) * P],
+                        rhs=x_codes[:, c, :].bitcast(FP8X4),
+                        rhs_scale=x_scales[:, c, :],
+                        start=(c == 0),
+                        stop=(c == PASSES_A - 1),
+                    )
+            lat_banks[n] = lat_ps
+
+        def copy_latent(n):
+            lat = lat_pool.tile([P, P, PACK], BF16, align_bytes=64)
+            nc.scalar.copy(out=lat[:], in_=lat_banks[n][:].rearrange("p m r -> p r m"))
+            lat_tiles[n] = lat
+
+        def quantise_latent(n):
+            lat_codes = lat_pool.tile([P, P], U32, align_bytes=64)
+            lat_scales = lat_pool.tile([P, P], U8, align_bytes=64)
+            nc.vector.quantize_mx(
+                out=lat_codes[:].bitcast(FP8X4), scales=lat_scales[:], in_=lat_tiles[n][:].rearrange("p r m -> p (r m)")
+            )
+            latq_tiles[n] = (lat_codes, lat_scales)
+
+        def second_matmul(n):
+            lat_codes, lat_scales = latq_tiles[n]
+            q_ps = q_psum.tile([P, HEADS, HEAD_DIM], F32)
+            nc.tensor.matmul_mx(
+                out=q_ps[:].rearrange("p h d -> p (h d)"),
+                lhsT=lat_codes[:].bitcast(FP8X4),
+                lhsT_scale=lat_scales[:],
+                rhs=wb_codes[:].bitcast(FP8X4),
+                rhs_scale=wb_scales[:],
+                start=True,
+                stop=True,
+            )
+            q_banks[n] = q_ps
+
+        def copy_nope(n):
+            if n % STORE_TILES == 0:
+                o_sb = out_pool.tile([P, HEADS, STORE_TILES, HEAD_DIM], F32)
+                out_tiles[n // STORE_TILES] = o_sb
+            o_sb = out_tiles[n // STORE_TILES]
+            nc.scalar.copy(out=o_sb[:, :, n % STORE_TILES, 0:NOPE_DIM], in_=q_banks[n][:, :, 0:NOPE_DIM])
+
+        def rope_products(n):
+            t = n % TILES_PER_BATCH
+            rotated = q_banks[n][:, :, NOPE_DIM:HEAD_DIM]
+            pairs = rotated.rearrange("p h (i e) -> p h i e", e=2)
+            by_cos = rope_pool.tile([P, HEADS, ROPE_DIM], F32)
+            by_sin = rope_pool.tile([P, 2, HEADS, PAIRS], F32)
+            nc.vector.tensor_tensor(
+                out=by_cos[:],
+                in0=rotated,
+                in1=cos2[:, t].rearrange("p i e -> p (i e)").unsqueeze(1).to_broadcast([P, HEADS, ROPE_DIM]),
+                op=ALU.mult,
+            )
+            for e in range(2):
+                nc.vector.tensor_tensor(
+                    out=by_sin[:, e],
+                    in0=pairs[:, :, :, 1 - e],
+                    in1=sin_pm[:, t, e, :].unsqueeze(1).to_broadcast([P, HEADS, PAIRS]),
+                    op=ALU.mult,
+                )
+            rope_tiles[n] = (by_cos, by_sin)
+
+        def rope_sum(n):
+            by_cos, by_sin = rope_tiles[n]
+            o_sb = out_tiles[n // STORE_TILES]
+            nc.vector.tensor_tensor(
+                out=o_sb[:, :, n % STORE_TILES, NOPE_DIM:HEAD_DIM].rearrange("p h (i e) -> p h i e", e=2),
+                in0=by_cos[:].rearrange("p h (i e) -> p h i e", e=2),
+                in1=by_sin[:].rearrange("p e h i -> p h i e"),
+                op=ALU.add,
+            )
+
+        def store(n_last):
+            b, t_last = divmod(n_last, TILES_PER_BATCH)
+            t0 = t_last - (STORE_TILES - 1)
+            nc.sync.dma_start(
+                out=out[b].rearrange("h (r t) d -> r h t d", t=TILES_PER_BATCH)[:, :, t0 : t0 + STORE_TILES, :],
+                in_=out_tiles[n_last // STORE_TILES][:],
+            )
+
+        def live(n):
+            return 0 <= n < N_TILES
+
+        def step(s):
+            ahead = s + LEAD_TILES
+            if live(ahead):
+                if ahead % RUN_TILES == 0:
+                    for n in range(ahead, ahead + RUN_TILES):
+                        transpose_x(n)
+                copy_x(ahead)
+            if live(s):
+                first_matmul(s)
+                copy_latent(s)
+            if live(s - 2):
+                second_matmul(s - 2)
+                copy_nope(s - 2)
+            if live(s - 1):
+                quantise_latent(s - 1)
+            if live(s - 3):
+                rope_products(s - 3)
+            if live(ahead - 1):
+                quantise_x(ahead - 1)
+            if live(s - 3):
+                rope_sum(s - 3)
+                if (s - 3) % STORE_TILES == STORE_TILES - 1:
+                    store(s - 3)
+
+        for s in range(-LEAD_TILES, 1):
+            step(s)
+        prepare_wqb_and_cos()
+        for s in range(1, N_TILES + 3):
+            step(s)

@@ -19,6 +19,7 @@ BATCH, SEQ, D_MODEL, Q_LATENT = 2, 2048, 1024, 512
 HEADS, HEAD_DIM, NOPE_DIM = 4, 128, 64
 ROPE_DIM = HEAD_DIM - NOPE_DIM
 PAIRS = ROPE_DIM // 2
+HALF_Q = HEADS * NOPE_DIM
 ROPE_THETA = 10000.0
 
 K_PASS = P * PACK
@@ -26,11 +27,8 @@ PASSES_A = D_MODEL // K_PASS
 WORDS = D_MODEL // 2
 LATENT_BLOCKS = Q_LATENT // P
 TILES_PER_BATCH = SEQ // P
-N_TILES = BATCH * TILES_PER_BATCH
-LOAD_TILES = 2
-STORE_TILES = 2
-RUN_TILES = 2
-LEAD_TILES = 3
+UNIT = 2
+UNITS = BATCH * TILES_PER_BATCH // UNIT
 
 FLOPS = 2 * BATCH * SEQ * (D_MODEL * Q_LATENT + Q_LATENT * HEADS * HEAD_DIM)
 
@@ -40,255 +38,295 @@ def tile_mlaattention_pa_t_kernel(tc, hidden_states, Wqa, Wqb, out):
     with ExitStack() as ctx:
         ctx.enter_context(tc.manual_schedule())
         const = ctx.enter_context(tc.tile_pool(name="const", bufs=1))
-        x_pool = ctx.enter_context(tc.tile_pool(name="x", bufs=N_TILES // LOAD_TILES))
-        xg_pool = ctx.enter_context(tc.tile_pool(name="xg", bufs=4))
-        xq_pool = ctx.enter_context(tc.tile_pool(name="xq", bufs=LEAD_TILES + 2))
+        x_pool = ctx.enter_context(tc.tile_pool(name="x", bufs=UNITS))
+        xg_pool = ctx.enter_context(tc.tile_pool(name="xg", bufs=3))
+        xq_pool = ctx.enter_context(tc.tile_pool(name="xq", bufs=3))
         lat_pool = ctx.enter_context(tc.tile_pool(name="lat", bufs=3))
         rope_pool = ctx.enter_context(tc.tile_pool(name="rope", bufs=2))
         out_pool = ctx.enter_context(tc.tile_pool(name="outp", bufs=4))
         xt_psum = ctx.enter_context(tc.psum_pool(name="xt_psum", bufs=3))
         lat_psum = ctx.enter_context(tc.psum_pool(name="lat_psum", bufs=2))
-        q_psum = ctx.enter_context(tc.psum_pool(name="q_psum", bufs=3))
+        nope_psum = ctx.enter_context(tc.psum_pool(name="nope_psum", bufs=1))
+        rope_psum = ctx.enter_context(tc.psum_pool(name="rope_psum", bufs=2))
 
         wa_raw = const.tile([P, PASSES_A, PACK, Q_LATENT], BF16)
-        for c in range(PASSES_A):
-            nc.sync.dma_start(
-                out=wa_raw[:, c],
-                in_=Wqa[c * K_PASS : (c + 1) * K_PASS, :].rearrange("(p j) n -> p j n", j=PACK),
-            )
         wb_raw = const.tile([P, PACK, Q_LATENT], BF16)
         x_tiles = []
-        for g in range(N_TILES // LOAD_TILES):
-            b, t0 = divmod(g * LOAD_TILES, TILES_PER_BATCH)
-            x_sb = x_pool.tile([P, LOAD_TILES, D_MODEL], BF16)
+        for u in range(UNITS):
+            b, t0 = divmod(u * UNIT, TILES_PER_BATCH)
+            x_sb = x_pool.tile([P, UNIT, D_MODEL], BF16)
             nc.sync.dma_start(
                 out=x_sb[:],
-                in_=hidden_states[b].rearrange("(r t) k -> r t k", t=TILES_PER_BATCH)[:, t0 : t0 + LOAD_TILES, :],
+                in_=hidden_states[b].rearrange("(r t) k -> r t k", t=TILES_PER_BATCH)[:, t0 : t0 + UNIT, :],
             )
             x_tiles.append(x_sb)
-            if g == 1:
+            if u == 0:
+                for c in range(PASSES_A):
+                    nc.sync.dma_start(
+                        out=wa_raw[:, c],
+                        in_=Wqa[c * K_PASS : (c + 1) * K_PASS, :].rearrange("(p j) n -> p j n", j=PACK),
+                    )
+            if u == 1:
                 nc.sync.dma_start(out=wb_raw[:], in_=Wqb.rearrange("(p j) n -> p j n", j=PACK))
 
+        pos = const.tile([P, TILES_PER_BATCH, 1], F32)
+        nc.gpsimd.iota(
+            pos[:].rearrange("p t o -> p (t o)"),
+            pattern=[[1, TILES_PER_BATCH]],
+            base=0,
+            channel_multiplier=TILES_PER_BATCH,
+            allow_small_or_imprecise_dtypes=True,
+        )
         ident = const.tile([P, P], F32)
         make_identity(nc, ident[:])
-        pos_i = const.tile([P, TILES_PER_BATCH], I32)
-        nc.gpsimd.iota(pos_i[:], pattern=[[1, TILES_PER_BATCH]], base=0, channel_multiplier=TILES_PER_BATCH)
 
         warm = const.tile([P, 2], F32)
         nc.vector.memset(warm[:], 0.0)
         nc.scalar.activation(out=warm[:, 1:2], in_=warm[:, 0:1], func=FUNC.Sin)
 
-        pos_f = const.tile([P, TILES_PER_BATCH], F32)
-        nc.vector.tensor_copy(out=pos_f[:], in_=pos_i[:])
-        turns = const.tile([P, PAIRS, TILES_PER_BATCH], F32)
-        for i in range(PAIRS):
+        turns = const.tile([P, TILES_PER_BATCH, PAIRS], F32)
+        nc.vector.tensor_scalar_mul(out=turns[:, :, 0:1], in0=pos[:], scalar1=1.0 / (2.0 * math.pi))
+        known = 1
+        while known < PAIRS:
             nc.vector.tensor_scalar_mul(
-                out=turns[:, i, :], in0=pos_f[:], scalar1=ROPE_THETA ** (-2.0 * i / ROPE_DIM) / (2.0 * math.pi)
+                out=turns[:, :, known : 2 * known],
+                in0=turns[:, :, 0:known],
+                scalar1=ROPE_THETA ** (-2.0 * known / ROPE_DIM),
             )
-        turns_flat = turns[:].rearrange("p i t -> p (i t)")
-        whole_i = const.tile([P, PAIRS * TILES_PER_BATCH], I32)
+            known *= 2
+        turns_flat = turns[:].rearrange("p t i -> p (t i)")
+        whole_i = const.tile([P, TILES_PER_BATCH * PAIRS], I32)
         nc.vector.tensor_copy(out=whole_i[:], in_=turns_flat)
-        whole_f = const.tile([P, PAIRS * TILES_PER_BATCH], F32)
+        whole_f = const.tile([P, TILES_PER_BATCH * PAIRS], F32)
         nc.vector.tensor_copy(out=whole_f[:], in_=whole_i[:])
-        left = const.tile([P, PAIRS * TILES_PER_BATCH], F32)
+        left = const.tile([P, TILES_PER_BATCH * PAIRS], F32)
         nc.vector.tensor_tensor(out=left[:], in0=turns_flat, in1=whole_f[:], op=ALU.subtract)
-        minus = const.tile([P, PAIRS, TILES_PER_BATCH], F32)
-        minus_flat = minus[:].rearrange("p i t -> p (i t)")
+        minus = const.tile([P, TILES_PER_BATCH * PAIRS], F32)
         nc.vector.scalar_tensor_tensor(
-            out=minus_flat, in0=left[:], scalar=0.5, in1=left[:], op0=ALU.is_gt, op1=ALU.subtract
+            out=minus[:], in0=left[:], scalar=0.5, in1=left[:], op0=ALU.is_gt, op1=ALU.subtract
         )
-        sin_pm = const.tile([P, TILES_PER_BATCH, 2, PAIRS], F32)
-        minus_ti = minus[:].rearrange("p i t -> p t i")
-        nc.scalar.activation(out=sin_pm[:, :, 0, :], in_=minus_ti, func=FUNC.Sin, scale=2.0 * math.pi)
-        nc.scalar.activation(out=sin_pm[:, :, 1, :], in_=minus_ti, func=FUNC.Sin, scale=-2.0 * math.pi)
-        half_sin = const.tile([P, PAIRS * TILES_PER_BATCH], F32)
-        nc.scalar.activation(out=half_sin[:], in_=minus_flat, func=FUNC.Sin, scale=math.pi)
-        twice_sq = const.tile([P, PAIRS, TILES_PER_BATCH], F32)
-        nc.scalar.activation(
-            out=twice_sq[:].rearrange("p i t -> p (i t)"), in_=half_sin[:], func=FUNC.Square, scale=math.sqrt(2.0)
-        )
-        cos2 = const.tile([P, TILES_PER_BATCH, PAIRS, 2], F32)
 
-        wa_grouped = const.tile([P, PASSES_A, Q_LATENT, PACK], BF16, align_bytes=64)
-        wa_codes = const.tile([P, PASSES_A, Q_LATENT], U32, align_bytes=64)
-        wa_scales = const.tile([P, PASSES_A, Q_LATENT], U8, align_bytes=64)
-        for c in range(PASSES_A):
-            nc.vector.tensor_copy(
-                out=wa_grouped[:, c].rearrange("p (m q) t -> p m q t", m=LATENT_BLOCKS),
-                in_=wa_raw[:, c].rearrange("p t (q m) -> p m q t", m=LATENT_BLOCKS),
-            )
-        for c in range(PASSES_A):
-            nc.vector.quantize_mx(
-                out=wa_codes[:, c, :].bitcast(FP8X4),
-                scales=wa_scales[:, c, :],
-                in_=wa_grouped[:, c].rearrange("p n t -> p (n t)"),
-            )
-        wb_grouped = const.tile([P, Q_LATENT, PACK], BF16, align_bytes=64)
-        wb_codes = const.tile([P, Q_LATENT], U32, align_bytes=64)
-        wb_scales = const.tile([P, Q_LATENT], U8, align_bytes=64)
+        signed_sin = const.tile([P, TILES_PER_BATCH * PAIRS, 2], F32)
+        half_sin = const.tile([P, TILES_PER_BATCH * PAIRS], F32)
+        twice_sq = const.tile([P, TILES_PER_BATCH * PAIRS], F32)
+        cos2 = const.tile([P, TILES_PER_BATCH * PAIRS, 2], F32)
 
-        def prepare_wqb_and_cos():
-            nc.vector.tensor_copy(out=wb_grouped[:], in_=wb_raw[:].rearrange("p j n -> p n j"))
+        def make_sines():
+            nc.scalar.activation(out=signed_sin[:, :, 0], in_=minus[:], func=FUNC.Sin, scale=2.0 * math.pi)
+            nc.scalar.activation(out=signed_sin[:, :, 1], in_=minus[:], func=FUNC.Sin, scale=-2.0 * math.pi)
+
+        def make_squares():
+            nc.scalar.activation(out=half_sin[:], in_=minus[:], func=FUNC.Sin, scale=math.pi)
+            nc.scalar.activation(out=twice_sq[:], in_=half_sin[:], func=FUNC.Square, scale=math.sqrt(2.0))
+
+        def make_cosines():
             nc.vector.tensor_scalar(
                 out=cos2[:],
-                in0=twice_sq[:].rearrange("p i t -> p t i").unsqueeze(3).to_broadcast([P, TILES_PER_BATCH, PAIRS, 2]),
+                in0=twice_sq[:].unsqueeze(2).to_broadcast([P, TILES_PER_BATCH * PAIRS, 2]),
                 scalar1=-1.0,
                 scalar2=1.0,
                 op0=ALU.mult,
                 op1=ALU.add,
             )
+
+        wa_grouped = const.tile([P, LATENT_BLOCKS, PASSES_A, P, PACK], BF16, align_bytes=64)
+        wa_codes = const.tile([P, LATENT_BLOCKS, PASSES_A, P], U32, align_bytes=64)
+        wa_scales = const.tile([P, LATENT_BLOCKS, PASSES_A, P], U8, align_bytes=64)
+
+        def group_wqa(m):
+            nc.vector.tensor_copy(
+                out=wa_grouped[:, m],
+                in_=wa_raw[:].rearrange("p c t (q m) -> p m c q t", m=LATENT_BLOCKS)[:, m],
+            )
+
+        def quantise_wqa(m):
             nc.vector.quantize_mx(
-                out=wb_codes[:].bitcast(FP8X4), scales=wb_scales[:], in_=wb_grouped[:].rearrange("p n j -> p (n j)")
+                out=wa_codes[:, m].rearrange("p c q -> p (c q)").bitcast(FP8X4),
+                scales=wa_scales[:, m].rearrange("p c q -> p (c q)"),
+                in_=wa_grouped[:, m].rearrange("p c q t -> p (c q t)"),
+            )
+
+        wb_grouped = const.tile([P, 2, HEADS, NOPE_DIM, PACK], BF16, align_bytes=64)
+        wb_codes = const.tile([P, 2, HALF_Q], U32, align_bytes=64)
+        wb_scales = const.tile([P, 2, HALF_Q], U8, align_bytes=64)
+
+        def group_wqb(s):
+            nc.vector.tensor_copy(
+                out=wb_grouped[:, s],
+                in_=wb_raw[:].rearrange("p j (h s d) -> p s h d j", h=HEADS, s=2)[:, s],
+            )
+
+        def quantise_wqb():
+            nc.vector.quantize_mx(
+                out=wb_codes[:].rearrange("p s n -> p (s n)").bitcast(FP8X4),
+                scales=wb_scales[:].rearrange("p s n -> p (s n)"),
+                in_=wb_grouped[:].rearrange("p s h d j -> p (s h d j)"),
             )
 
         xt_banks, xg_tiles, xq_tiles = {}, {}, {}
         lat_banks, lat_tiles, latq_tiles = {}, {}, {}
-        q_banks, rope_tiles, out_tiles = {}, {}, {}
+        nope_banks, rope_banks, rope_tiles, out_tiles = {}, {}, {}, {}
 
-        def transpose_x(n):
-            words = x_tiles[n // LOAD_TILES][:, n % LOAD_TILES, :].bitcast(F32)
-            xt = xt_psum.tile([P, WORDS // P, P], F32)
-            for w in range(WORDS // P):
-                first = 2 * P * (w // 2) + w % 2
-                nc.tensor.transpose(xt[:, w, :], words[:, first : 2 * P * (w // 2 + 1) : 2], ident[:])
-            xt_banks[n] = xt
+        def transpose_x(u):
+            for i in range(UNIT):
+                words = x_tiles[u][:, i, :].bitcast(F32)
+                xt = xt_psum.tile([P, WORDS // P, P], F32)
+                for w in range(WORDS // P):
+                    first = 2 * P * (w // 2) + w % 2
+                    nc.tensor.transpose(xt[:, w, :], words[:, first : 2 * P * (w // 2 + 1) : 2], ident[:])
+                xt_banks[u, i] = xt
 
-        def copy_x(n):
-            xg = xg_pool.tile([P, PASSES_A, P, PACK], BF16, align_bytes=64)
-            nc.scalar.copy(
-                out=xg[:].rearrange("p c r t -> p c (r t)").bitcast(F32).rearrange("p c (r u) -> p c r u", u=2),
-                in_=xt_banks[n][:].rearrange("p (c u) r -> p c r u", u=2),
-            )
-            xg_tiles[n] = xg
+        def copy_x(u):
+            xg = xg_pool.tile([P, UNIT, PASSES_A, P, PACK], BF16, align_bytes=64)
+            for i in range(UNIT):
+                nc.scalar.copy(
+                    out=xg[:, i].rearrange("p c r t -> p c (r t)").bitcast(F32).rearrange("p c (r v) -> p c r v", v=2),
+                    in_=xt_banks[u, i][:].rearrange("p (c v) r -> p c r v", v=2),
+                )
+            xg_tiles[u] = xg
 
-        def quantise_x(n):
-            x_codes = xq_pool.tile([P, PASSES_A, P], U32, align_bytes=64)
-            x_scales = xq_pool.tile([P, PASSES_A, P], U8, align_bytes=64)
+        def quantise_x(u):
+            x_codes = xq_pool.tile([P, UNIT, PASSES_A, P], U32, align_bytes=64)
+            x_scales = xq_pool.tile([P, UNIT, PASSES_A, P], U8, align_bytes=64)
             nc.vector.quantize_mx(
-                out=x_codes[:].rearrange("p c r -> p (c r)").bitcast(FP8X4),
-                scales=x_scales[:].rearrange("p c r -> p (c r)"),
-                in_=xg_tiles[n][:].rearrange("p c r t -> p (c r t)"),
+                out=x_codes[:].rearrange("p i c r -> p (i c r)").bitcast(FP8X4),
+                scales=x_scales[:].rearrange("p i c r -> p (i c r)"),
+                in_=xg_tiles[u][:].rearrange("p i c r t -> p (i c r t)"),
             )
-            xq_tiles[n] = (x_codes, x_scales)
+            xq_tiles[u] = (x_codes, x_scales)
 
-        def first_matmul(n):
-            x_codes, x_scales = xq_tiles[n]
-            lat_ps = lat_psum.tile([P, LATENT_BLOCKS, P], F32)
-            for m in range(LATENT_BLOCKS):
-                for c in range(PASSES_A):
+        def first_matmul(u):
+            x_codes, x_scales = xq_tiles[u]
+            for i in range(UNIT):
+                lat_ps = lat_psum.tile([P, LATENT_BLOCKS, P], F32)
+                for m in range(LATENT_BLOCKS):
+                    for c in range(PASSES_A):
+                        nc.tensor.matmul_mx(
+                            out=lat_ps[:, m, :],
+                            lhsT=wa_codes[:, m, c, :].bitcast(FP8X4),
+                            lhsT_scale=wa_scales[:, m, c, :],
+                            rhs=x_codes[:, i, c, :].bitcast(FP8X4),
+                            rhs_scale=x_scales[:, i, c, :],
+                            start=(c == 0),
+                            stop=(c == PASSES_A - 1),
+                        )
+                lat_banks[u, i] = lat_ps
+
+        def copy_latent(u):
+            lat = lat_pool.tile([P, UNIT, P, PACK], BF16, align_bytes=64)
+            for i in range(UNIT):
+                nc.scalar.copy(out=lat[:, i], in_=lat_banks[u, i][:].rearrange("p m r -> p r m"))
+            lat_tiles[u] = lat
+
+        def quantise_latent(u):
+            lat_codes = lat_pool.tile([P, UNIT, P], U32, align_bytes=64)
+            lat_scales = lat_pool.tile([P, UNIT, P], U8, align_bytes=64)
+            nc.vector.quantize_mx(
+                out=lat_codes[:].rearrange("p i r -> p (i r)").bitcast(FP8X4),
+                scales=lat_scales[:].rearrange("p i r -> p (i r)"),
+                in_=lat_tiles[u][:].rearrange("p i r m -> p (i r m)"),
+            )
+            latq_tiles[u] = (lat_codes, lat_scales)
+
+        def second_matmul(u):
+            lat_codes, lat_scales = latq_tiles[u]
+            nope_ps = nope_psum.tile([P, UNIT, HALF_Q], F32)
+            rope_ps = rope_psum.tile([P, UNIT, HALF_Q], F32)
+            for i in range(UNIT):
+                for s, q_ps in enumerate((nope_ps, rope_ps)):
                     nc.tensor.matmul_mx(
-                        out=lat_ps[:, m, :],
-                        lhsT=wa_codes[:, c, m * P : (m + 1) * P].bitcast(FP8X4),
-                        lhsT_scale=wa_scales[:, c, m * P : (m + 1) * P],
-                        rhs=x_codes[:, c, :].bitcast(FP8X4),
-                        rhs_scale=x_scales[:, c, :],
-                        start=(c == 0),
-                        stop=(c == PASSES_A - 1),
+                        out=q_ps[:, i, :],
+                        lhsT=lat_codes[:, i, :].bitcast(FP8X4),
+                        lhsT_scale=lat_scales[:, i, :],
+                        rhs=wb_codes[:, s, :].bitcast(FP8X4),
+                        rhs_scale=wb_scales[:, s, :],
+                        start=True,
+                        stop=True,
                     )
-            lat_banks[n] = lat_ps
+            nope_banks[u], rope_banks[u] = nope_ps, rope_ps
 
-        def copy_latent(n):
-            lat = lat_pool.tile([P, P, PACK], BF16, align_bytes=64)
-            nc.scalar.copy(out=lat[:], in_=lat_banks[n][:].rearrange("p m r -> p r m"))
-            lat_tiles[n] = lat
-
-        def quantise_latent(n):
-            lat_codes = lat_pool.tile([P, P], U32, align_bytes=64)
-            lat_scales = lat_pool.tile([P, P], U8, align_bytes=64)
-            nc.vector.quantize_mx(
-                out=lat_codes[:].bitcast(FP8X4), scales=lat_scales[:], in_=lat_tiles[n][:].rearrange("p r m -> p (r m)")
+        def copy_nope(u):
+            o_sb = out_pool.tile([P, HEADS, UNIT, HEAD_DIM], F32)
+            nc.scalar.copy(
+                out=o_sb[:, :, :, 0:NOPE_DIM].rearrange("p h i d -> p i h d"),
+                in_=nope_banks[u][:].rearrange("p i (h d) -> p i h d", h=HEADS),
             )
-            latq_tiles[n] = (lat_codes, lat_scales)
+            out_tiles[u] = o_sb
 
-        def second_matmul(n):
-            lat_codes, lat_scales = latq_tiles[n]
-            q_ps = q_psum.tile([P, HEADS, HEAD_DIM], F32)
-            nc.tensor.matmul_mx(
-                out=q_ps[:].rearrange("p h d -> p (h d)"),
-                lhsT=lat_codes[:].bitcast(FP8X4),
-                lhsT_scale=lat_scales[:],
-                rhs=wb_codes[:].bitcast(FP8X4),
-                rhs_scale=wb_scales[:],
-                start=True,
-                stop=True,
-            )
-            q_banks[n] = q_ps
-
-        def copy_nope(n):
-            if n % STORE_TILES == 0:
-                o_sb = out_pool.tile([P, HEADS, STORE_TILES, HEAD_DIM], F32)
-                out_tiles[n // STORE_TILES] = o_sb
-            o_sb = out_tiles[n // STORE_TILES]
-            nc.scalar.copy(out=o_sb[:, :, n % STORE_TILES, 0:NOPE_DIM], in_=q_banks[n][:, :, 0:NOPE_DIM])
-
-        def rope_products(n):
-            t = n % TILES_PER_BATCH
-            rotated = q_banks[n][:, :, NOPE_DIM:HEAD_DIM]
-            pairs = rotated.rearrange("p h (i e) -> p h i e", e=2)
-            by_cos = rope_pool.tile([P, HEADS, ROPE_DIM], F32)
-            by_sin = rope_pool.tile([P, 2, HEADS, PAIRS], F32)
+        def rope_products(u):
+            t0 = u * UNIT % TILES_PER_BATCH
+            here = slice(t0 * PAIRS, (t0 + UNIT) * PAIRS)
+            shape = [P, UNIT, HEADS, PAIRS, 2]
+            rotated = rope_banks[u][:].rearrange("p i (h a e) -> p i h a e", h=HEADS, e=2)
+            by_cos = rope_pool.tile(shape, F32)
+            by_sin = rope_pool.tile(shape, F32)
             nc.vector.tensor_tensor(
                 out=by_cos[:],
                 in0=rotated,
-                in1=cos2[:, t].rearrange("p i e -> p (i e)").unsqueeze(1).to_broadcast([P, HEADS, ROPE_DIM]),
+                in1=cos2[:, here, :].rearrange("p (i a) e -> p i a e", i=UNIT).unsqueeze(2).to_broadcast(shape),
                 op=ALU.mult,
             )
-            for e in range(2):
-                nc.vector.tensor_tensor(
-                    out=by_sin[:, e],
-                    in0=pairs[:, :, :, 1 - e],
-                    in1=sin_pm[:, t, e, :].unsqueeze(1).to_broadcast([P, HEADS, PAIRS]),
-                    op=ALU.mult,
-                )
-            rope_tiles[n] = (by_cos, by_sin)
-
-        def rope_sum(n):
-            by_cos, by_sin = rope_tiles[n]
-            o_sb = out_tiles[n // STORE_TILES]
             nc.vector.tensor_tensor(
-                out=o_sb[:, :, n % STORE_TILES, NOPE_DIM:HEAD_DIM].rearrange("p h (i e) -> p h i e", e=2),
-                in0=by_cos[:].rearrange("p h (i e) -> p h i e", e=2),
-                in1=by_sin[:].rearrange("p e h i -> p h i e"),
+                out=by_sin[:],
+                in0=rotated[:, :, :, :, ::-1],
+                in1=signed_sin[:, here, :].rearrange("p (i a) e -> p i a e", i=UNIT).unsqueeze(2).to_broadcast(shape),
+                op=ALU.mult,
+            )
+            rope_tiles[u] = (by_cos, by_sin)
+
+        def rope_sum(u):
+            by_cos, by_sin = rope_tiles[u]
+            nc.vector.tensor_tensor(
+                out=out_tiles[u][:, :, :, NOPE_DIM:HEAD_DIM].rearrange("p h i d -> p i h d"),
+                in0=by_cos[:].rearrange("p i h a e -> p i h (a e)"),
+                in1=by_sin[:].rearrange("p i h a e -> p i h (a e)"),
                 op=ALU.add,
             )
 
-        def store(n_last):
-            b, t_last = divmod(n_last, TILES_PER_BATCH)
-            t0 = t_last - (STORE_TILES - 1)
+        def store(u):
+            b, t0 = divmod(u * UNIT, TILES_PER_BATCH)
             nc.sync.dma_start(
-                out=out[b].rearrange("h (r t) d -> r h t d", t=TILES_PER_BATCH)[:, :, t0 : t0 + STORE_TILES, :],
-                in_=out_tiles[n_last // STORE_TILES][:],
+                out=out[b].rearrange("h (r t) d -> r h t d", t=TILES_PER_BATCH)[:, :, t0 : t0 + UNIT, :],
+                in_=out_tiles[u][:],
             )
 
-        def live(n):
-            return 0 <= n < N_TILES
+        def live(u):
+            return 0 <= u < UNITS
 
         def step(s):
-            ahead = s + LEAD_TILES
-            if live(ahead):
-                if ahead % RUN_TILES == 0:
-                    for n in range(ahead, ahead + RUN_TILES):
-                        transpose_x(n)
-                copy_x(ahead)
+            if live(s + 2):
+                transpose_x(s + 2)
+                copy_x(s + 2)
             if live(s):
                 first_matmul(s)
                 copy_latent(s)
-            if live(s - 2):
-                second_matmul(s - 2)
-                copy_nope(s - 2)
             if live(s - 1):
                 quantise_latent(s - 1)
-            if live(s - 3):
-                rope_products(s - 3)
-            if live(ahead - 1):
-                quantise_x(ahead - 1)
-            if live(s - 3):
-                rope_sum(s - 3)
-                if (s - 3) % STORE_TILES == STORE_TILES - 1:
-                    store(s - 3)
+                second_matmul(s - 1)
+                copy_nope(s - 1)
+            if live(s - 2):
+                rope_products(s - 2)
+            if live(s + 1):
+                quantise_x(s + 1)
+            if live(s - 2):
+                rope_sum(s - 2)
+                store(s - 2)
 
-        for s in range(-LEAD_TILES, 1):
-            step(s)
-        prepare_wqb_and_cos()
-        for s in range(1, N_TILES + 3):
+        step(-2)
+        make_sines()
+        group_wqa(0)
+        group_wqa(1)
+        quantise_wqa(0)
+        step(-1)
+        make_squares()
+        group_wqa(2)
+        quantise_wqa(1)
+        group_wqa(3)
+        quantise_wqa(2)
+        group_wqb(0)
+        quantise_wqa(3)
+        group_wqb(1)
+        make_cosines()
+        quantise_wqb()
+        for s in range(0, UNITS + 2):
             step(s)

@@ -27,8 +27,12 @@ PASSES_A = D_MODEL // K_PASS
 WORDS = D_MODEL // 2
 LATENT_BLOCKS = Q_LATENT // P
 TILES_PER_BATCH = SEQ // P
+N_TILES = BATCH * TILES_PER_BATCH
 UNIT = 2
-UNITS = BATCH * TILES_PER_BATCH // UNIT
+UNIT_TILES = [(n, n + 1) for n in range(0, N_TILES - UNIT, UNIT)] + [(N_TILES - 2,), (N_TILES - 1,)]
+UNITS = len(UNIT_TILES)
+ANGLES = TILES_PER_BATCH * PAIRS
+LOADS = N_TILES // UNIT
 
 FLOPS = 2 * BATCH * SEQ * (D_MODEL * Q_LATENT + Q_LATENT * HEADS * HEAD_DIM)
 
@@ -38,7 +42,7 @@ def tile_mlaattention_pa_t_kernel(tc, hidden_states, Wqa, Wqb, out):
     with ExitStack() as ctx:
         ctx.enter_context(tc.manual_schedule())
         const = ctx.enter_context(tc.tile_pool(name="const", bufs=1))
-        x_pool = ctx.enter_context(tc.tile_pool(name="x", bufs=UNITS))
+        x_pool = ctx.enter_context(tc.tile_pool(name="x", bufs=LOADS))
         xg_pool = ctx.enter_context(tc.tile_pool(name="xg", bufs=3))
         xq_pool = ctx.enter_context(tc.tile_pool(name="xq", bufs=3))
         lat_pool = ctx.enter_context(tc.tile_pool(name="lat", bufs=3))
@@ -52,26 +56,26 @@ def tile_mlaattention_pa_t_kernel(tc, hidden_states, Wqa, Wqb, out):
         wa_raw = const.tile([P, PASSES_A, PACK, Q_LATENT], BF16)
         wb_raw = const.tile([P, PACK, Q_LATENT], BF16)
         x_tiles = []
-        for u in range(UNITS):
-            b, t0 = divmod(u * UNIT, TILES_PER_BATCH)
+        for g in range(LOADS):
+            b, t0 = divmod(g * UNIT, TILES_PER_BATCH)
             x_sb = x_pool.tile([P, UNIT, D_MODEL], BF16)
             nc.sync.dma_start(
                 out=x_sb[:],
                 in_=hidden_states[b].rearrange("(r t) k -> r t k", t=TILES_PER_BATCH)[:, t0 : t0 + UNIT, :],
             )
             x_tiles.append(x_sb)
-            if u == 0:
+            if g == 0:
                 for c in range(PASSES_A):
                     nc.sync.dma_start(
                         out=wa_raw[:, c],
                         in_=Wqa[c * K_PASS : (c + 1) * K_PASS, :].rearrange("(p j) n -> p j n", j=PACK),
                     )
-            if u == 1:
+            if g == 1:
                 nc.sync.dma_start(out=wb_raw[:], in_=Wqb.rearrange("(p j) n -> p j n", j=PACK))
 
-        pos = const.tile([P, TILES_PER_BATCH, 1], F32)
+        pos = const.tile([P, TILES_PER_BATCH], F32)
         nc.gpsimd.iota(
-            pos[:].rearrange("p t o -> p (t o)"),
+            pos[:],
             pattern=[[1, TILES_PER_BATCH]],
             base=0,
             channel_multiplier=TILES_PER_BATCH,
@@ -84,45 +88,46 @@ def tile_mlaattention_pa_t_kernel(tc, hidden_states, Wqa, Wqb, out):
         nc.vector.memset(warm[:], 0.0)
         nc.scalar.activation(out=warm[:, 1:2], in_=warm[:, 0:1], func=FUNC.Sin)
 
-        turns = const.tile([P, TILES_PER_BATCH, PAIRS], F32)
-        nc.vector.tensor_scalar_mul(out=turns[:, :, 0:1], in0=pos[:], scalar1=1.0 / (2.0 * math.pi))
+        turns = const.tile([P, TILES_PER_BATCH, PAIRS, 2], F32)
+        for e, sign in enumerate((-1.0, 1.0)):
+            nc.vector.tensor_scalar_mul(out=turns[:, :, 0, e], in0=pos[:], scalar1=sign / (2.0 * math.pi))
         known = 1
         while known < PAIRS:
             nc.vector.tensor_scalar_mul(
-                out=turns[:, :, known : 2 * known],
-                in0=turns[:, :, 0:known],
+                out=turns[:, :, known : 2 * known, :],
+                in0=turns[:, :, 0:known, :],
                 scalar1=ROPE_THETA ** (-2.0 * known / ROPE_DIM),
             )
             known *= 2
-        turns_flat = turns[:].rearrange("p t i -> p (t i)")
-        whole_i = const.tile([P, TILES_PER_BATCH * PAIRS], I32)
-        nc.vector.tensor_copy(out=whole_i[:], in_=turns_flat)
-        whole_f = const.tile([P, TILES_PER_BATCH * PAIRS], F32)
-        nc.vector.tensor_copy(out=whole_f[:], in_=whole_i[:])
-        left = const.tile([P, TILES_PER_BATCH * PAIRS], F32)
-        nc.vector.tensor_tensor(out=left[:], in0=turns_flat, in1=whole_f[:], op=ALU.subtract)
-        minus = const.tile([P, TILES_PER_BATCH * PAIRS], F32)
-        nc.vector.scalar_tensor_tensor(
-            out=minus[:], in0=left[:], scalar=0.5, in1=left[:], op0=ALU.is_gt, op1=ALU.subtract
+        turns_flat = turns[:].rearrange("p t i e -> p (t i e)")
+        whole = const.tile([P, ANGLES * 2], I32)
+        nc.vector.tensor_copy(out=whole[:], in_=turns_flat)
+        left = const.tile([P, ANGLES, 2], F32)
+        nc.vector.tensor_tensor(
+            out=left[:].rearrange("p a e -> p (a e)"), in0=turns_flat, in1=whole[:], op=ALU.subtract
         )
 
-        signed_sin = const.tile([P, TILES_PER_BATCH * PAIRS, 2], F32)
-        half_sin = const.tile([P, TILES_PER_BATCH * PAIRS], F32)
-        twice_sq = const.tile([P, TILES_PER_BATCH * PAIRS], F32)
-        cos2 = const.tile([P, TILES_PER_BATCH * PAIRS, 2], F32)
+        signed_sin = const.tile([P, ANGLES, 2], F32)
+        half_sin = const.tile([P, ANGLES], F32)
+        twice_sq = const.tile([P, ANGLES], F32)
+        cos2 = const.tile([P, ANGLES, 2], F32)
 
         def make_sines():
-            nc.scalar.activation(out=signed_sin[:, :, 0], in_=minus[:], func=FUNC.Sin, scale=2.0 * math.pi)
-            nc.scalar.activation(out=signed_sin[:, :, 1], in_=minus[:], func=FUNC.Sin, scale=-2.0 * math.pi)
+            nc.scalar.activation(
+                out=signed_sin[:].rearrange("p a e -> p (a e)"),
+                in_=left[:].rearrange("p a e -> p (a e)"),
+                func=FUNC.Sin,
+                scale=2.0 * math.pi,
+            )
 
         def make_squares():
-            nc.scalar.activation(out=half_sin[:], in_=minus[:], func=FUNC.Sin, scale=math.pi)
+            nc.scalar.activation(out=half_sin[:], in_=left[:, :, 1], func=FUNC.Sin, scale=math.pi)
             nc.scalar.activation(out=twice_sq[:], in_=half_sin[:], func=FUNC.Square, scale=math.sqrt(2.0))
 
         def make_cosines():
             nc.vector.tensor_scalar(
                 out=cos2[:],
-                in0=twice_sq[:].unsqueeze(2).to_broadcast([P, TILES_PER_BATCH * PAIRS, 2]),
+                in0=twice_sq[:].unsqueeze(2).to_broadcast([P, ANGLES, 2]),
                 scalar1=-1.0,
                 scalar2=1.0,
                 op0=ALU.mult,
@@ -133,17 +138,17 @@ def tile_mlaattention_pa_t_kernel(tc, hidden_states, Wqa, Wqb, out):
         wa_codes = const.tile([P, LATENT_BLOCKS, PASSES_A, P], U32, align_bytes=64)
         wa_scales = const.tile([P, LATENT_BLOCKS, PASSES_A, P], U8, align_bytes=64)
 
-        def group_wqa(m):
-            nc.vector.tensor_copy(
-                out=wa_grouped[:, m],
-                in_=wa_raw[:].rearrange("p c t (q m) -> p m c q t", m=LATENT_BLOCKS)[:, m],
+        def group_wqa(copy, c, m0, m1):
+            copy(
+                out=wa_grouped[:, m0:m1, c],
+                in_=wa_raw[:, c].rearrange("p t (q m) -> p m q t", m=LATENT_BLOCKS)[:, m0:m1],
             )
 
-        def quantise_wqa(m):
+        def quantise_wqa(m0, m1):
             nc.vector.quantize_mx(
-                out=wa_codes[:, m].rearrange("p c q -> p (c q)").bitcast(FP8X4),
-                scales=wa_scales[:, m].rearrange("p c q -> p (c q)"),
-                in_=wa_grouped[:, m].rearrange("p c q t -> p (c q t)"),
+                out=wa_codes[:, m0:m1].rearrange("p m c q -> p (m c q)").bitcast(FP8X4),
+                scales=wa_scales[:, m0:m1].rearrange("p m c q -> p (m c q)"),
+                in_=wa_grouped[:, m0:m1].rearrange("p m c q t -> p (m c q t)"),
             )
 
         wb_grouped = const.tile([P, 2, HEADS, NOPE_DIM, PACK], BF16, align_bytes=64)
@@ -168,8 +173,8 @@ def tile_mlaattention_pa_t_kernel(tc, hidden_states, Wqa, Wqb, out):
         nope_banks, rope_banks, rope_tiles, out_tiles = {}, {}, {}, {}
 
         def transpose_x(u):
-            for i in range(UNIT):
-                words = x_tiles[u][:, i, :].bitcast(F32)
+            for i, n in enumerate(UNIT_TILES[u]):
+                words = x_tiles[n // UNIT][:, n % UNIT, :].bitcast(F32)
                 xt = xt_psum.tile([P, WORDS // P, P], F32)
                 for w in range(WORDS // P):
                     first = 2 * P * (w // 2) + w % 2
@@ -178,7 +183,7 @@ def tile_mlaattention_pa_t_kernel(tc, hidden_states, Wqa, Wqb, out):
 
         def copy_x(u):
             xg = xg_pool.tile([P, UNIT, PASSES_A, P, PACK], BF16, align_bytes=64)
-            for i in range(UNIT):
+            for i in range(len(UNIT_TILES[u])):
                 nc.scalar.copy(
                     out=xg[:, i].rearrange("p c r t -> p c (r t)").bitcast(F32).rearrange("p c (r v) -> p c r v", v=2),
                     in_=xt_banks[u, i][:].rearrange("p (c v) r -> p c r v", v=2),
@@ -186,18 +191,19 @@ def tile_mlaattention_pa_t_kernel(tc, hidden_states, Wqa, Wqb, out):
             xg_tiles[u] = xg
 
         def quantise_x(u):
+            size = len(UNIT_TILES[u])
             x_codes = xq_pool.tile([P, UNIT, PASSES_A, P], U32, align_bytes=64)
             x_scales = xq_pool.tile([P, UNIT, PASSES_A, P], U8, align_bytes=64)
             nc.vector.quantize_mx(
-                out=x_codes[:].rearrange("p i c r -> p (i c r)").bitcast(FP8X4),
-                scales=x_scales[:].rearrange("p i c r -> p (i c r)"),
-                in_=xg_tiles[u][:].rearrange("p i c r t -> p (i c r t)"),
+                out=x_codes[:, :size].rearrange("p i c r -> p (i c r)").bitcast(FP8X4),
+                scales=x_scales[:, :size].rearrange("p i c r -> p (i c r)"),
+                in_=xg_tiles[u][:, :size].rearrange("p i c r t -> p (i c r t)"),
             )
             xq_tiles[u] = (x_codes, x_scales)
 
         def first_matmul(u):
             x_codes, x_scales = xq_tiles[u]
-            for i in range(UNIT):
+            for i in range(len(UNIT_TILES[u])):
                 lat_ps = lat_psum.tile([P, LATENT_BLOCKS, P], F32)
                 for m in range(LATENT_BLOCKS):
                     for c in range(PASSES_A):
@@ -214,17 +220,18 @@ def tile_mlaattention_pa_t_kernel(tc, hidden_states, Wqa, Wqb, out):
 
         def copy_latent(u):
             lat = lat_pool.tile([P, UNIT, P, PACK], BF16, align_bytes=64)
-            for i in range(UNIT):
+            for i in range(len(UNIT_TILES[u])):
                 nc.scalar.copy(out=lat[:, i], in_=lat_banks[u, i][:].rearrange("p m r -> p r m"))
             lat_tiles[u] = lat
 
         def quantise_latent(u):
+            size = len(UNIT_TILES[u])
             lat_codes = lat_pool.tile([P, UNIT, P], U32, align_bytes=64)
             lat_scales = lat_pool.tile([P, UNIT, P], U8, align_bytes=64)
             nc.vector.quantize_mx(
-                out=lat_codes[:].rearrange("p i r -> p (i r)").bitcast(FP8X4),
-                scales=lat_scales[:].rearrange("p i r -> p (i r)"),
-                in_=lat_tiles[u][:].rearrange("p i r m -> p (i r m)"),
+                out=lat_codes[:, :size].rearrange("p i r -> p (i r)").bitcast(FP8X4),
+                scales=lat_scales[:, :size].rearrange("p i r -> p (i r)"),
+                in_=lat_tiles[u][:, :size].rearrange("p i r m -> p (i r m)"),
             )
             latq_tiles[u] = (lat_codes, lat_scales)
 
@@ -232,7 +239,7 @@ def tile_mlaattention_pa_t_kernel(tc, hidden_states, Wqa, Wqb, out):
             lat_codes, lat_scales = latq_tiles[u]
             nope_ps = nope_psum.tile([P, UNIT, HALF_Q], F32)
             rope_ps = rope_psum.tile([P, UNIT, HALF_Q], F32)
-            for i in range(UNIT):
+            for i in range(len(UNIT_TILES[u])):
                 for s, q_ps in enumerate((nope_ps, rope_ps)):
                     nc.tensor.matmul_mx(
                         out=q_ps[:, i, :],
@@ -246,57 +253,58 @@ def tile_mlaattention_pa_t_kernel(tc, hidden_states, Wqa, Wqb, out):
             nope_banks[u], rope_banks[u] = nope_ps, rope_ps
 
         def copy_nope(u):
+            size = len(UNIT_TILES[u])
             o_sb = out_pool.tile([P, HEADS, UNIT, HEAD_DIM], F32)
             nc.scalar.copy(
-                out=o_sb[:, :, :, 0:NOPE_DIM].rearrange("p h i d -> p i h d"),
-                in_=nope_banks[u][:].rearrange("p i (h d) -> p i h d", h=HEADS),
+                out=o_sb[:, :, :size, 0:NOPE_DIM].rearrange("p h i d -> p i h d"),
+                in_=nope_banks[u][:, :size].rearrange("p i (h d) -> p i h d", h=HEADS),
             )
             out_tiles[u] = o_sb
 
         def rope_products(u):
-            t0 = u * UNIT % TILES_PER_BATCH
-            here = slice(t0 * PAIRS, (t0 + UNIT) * PAIRS)
-            shape = [P, UNIT, HEADS, PAIRS, 2]
-            rotated = rope_banks[u][:].rearrange("p i (h a e) -> p i h a e", h=HEADS, e=2)
-            by_cos = rope_pool.tile(shape, F32)
-            by_sin = rope_pool.tile(shape, F32)
+            size = len(UNIT_TILES[u])
+            t0 = UNIT_TILES[u][0] % TILES_PER_BATCH
+            here = slice(t0 * PAIRS, (t0 + size) * PAIRS)
+            shape = [P, size, HEADS, PAIRS, 2]
+            rotated = rope_banks[u][:, :size].rearrange("p i (h a e) -> p i h a e", h=HEADS, e=2)
+            by_cos = rope_pool.tile([P, UNIT, HEADS, PAIRS, 2], F32)
+            by_sin = rope_pool.tile([P, UNIT, HEADS, PAIRS, 2], F32)
             nc.vector.tensor_tensor(
-                out=by_cos[:],
+                out=by_cos[:, :size],
                 in0=rotated,
-                in1=cos2[:, here, :].rearrange("p (i a) e -> p i a e", i=UNIT).unsqueeze(2).to_broadcast(shape),
+                in1=cos2[:, here, :].rearrange("p (i a) e -> p i a e", i=size).unsqueeze(2).to_broadcast(shape),
                 op=ALU.mult,
             )
             nc.vector.tensor_tensor(
-                out=by_sin[:],
+                out=by_sin[:, :size],
                 in0=rotated[:, :, :, :, ::-1],
-                in1=signed_sin[:, here, :].rearrange("p (i a) e -> p i a e", i=UNIT).unsqueeze(2).to_broadcast(shape),
+                in1=signed_sin[:, here, :].rearrange("p (i a) e -> p i a e", i=size).unsqueeze(2).to_broadcast(shape),
                 op=ALU.mult,
             )
             rope_tiles[u] = (by_cos, by_sin)
 
         def rope_sum(u):
+            size = len(UNIT_TILES[u])
             by_cos, by_sin = rope_tiles[u]
             nc.vector.tensor_tensor(
-                out=out_tiles[u][:, :, :, NOPE_DIM:HEAD_DIM].rearrange("p h i d -> p i h d"),
-                in0=by_cos[:].rearrange("p i h a e -> p i h (a e)"),
-                in1=by_sin[:].rearrange("p i h a e -> p i h (a e)"),
+                out=out_tiles[u][:, :, :size, NOPE_DIM:HEAD_DIM].rearrange("p h i d -> p i h d"),
+                in0=by_cos[:, :size].rearrange("p i h a e -> p i h (a e)"),
+                in1=by_sin[:, :size].rearrange("p i h a e -> p i h (a e)"),
                 op=ALU.add,
             )
 
         def store(u):
-            b, t0 = divmod(u * UNIT, TILES_PER_BATCH)
+            size = len(UNIT_TILES[u])
+            b, t0 = divmod(UNIT_TILES[u][0], TILES_PER_BATCH)
             nc.sync.dma_start(
-                out=out[b].rearrange("h (r t) d -> r h t d", t=TILES_PER_BATCH)[:, :, t0 : t0 + UNIT, :],
-                in_=out_tiles[u][:],
+                out=out[b].rearrange("h (r t) d -> r h t d", t=TILES_PER_BATCH)[:, :, t0 : t0 + size, :],
+                in_=out_tiles[u][:, :, :size, :],
             )
 
         def live(u):
             return 0 <= u < UNITS
 
-        def step(s):
-            if live(s + 2):
-                transpose_x(s + 2)
-                copy_x(s + 2)
+        def matmuls(s):
             if live(s):
                 first_matmul(s)
                 copy_latent(s)
@@ -304,6 +312,12 @@ def tile_mlaattention_pa_t_kernel(tc, hidden_states, Wqa, Wqb, out):
                 quantise_latent(s - 1)
                 second_matmul(s - 1)
                 copy_nope(s - 1)
+
+        def step(s):
+            matmuls(s)
+            if live(s + 2):
+                transpose_x(s + 2)
+                copy_x(s + 2)
             if live(s - 2):
                 rope_products(s - 2)
             if live(s + 1):
@@ -312,21 +326,25 @@ def tile_mlaattention_pa_t_kernel(tc, hidden_states, Wqa, Wqb, out):
                 rope_sum(s - 2)
                 store(s - 2)
 
-        step(-2)
+        transpose_x(0)
+        copy_x(0)
+        group_wqa(nc.vector.tensor_copy, 0, 0, 4)
+        group_wqa(nc.scalar.copy, 1, 2, 4)
+        group_wqa(nc.vector.tensor_copy, 1, 0, 2)
+        quantise_x(0)
         make_sines()
-        group_wqa(0)
-        group_wqa(1)
-        quantise_wqa(0)
-        step(-1)
-        make_squares()
-        group_wqa(2)
-        quantise_wqa(1)
-        group_wqa(3)
-        quantise_wqa(2)
+        quantise_wqa(0, 2)
+        quantise_wqa(2, 4)
+        transpose_x(1)
+        copy_x(1)
         group_wqb(0)
-        quantise_wqa(3)
+        matmuls(0)
+        make_squares()
+        quantise_x(1)
         group_wqb(1)
-        make_cosines()
         quantise_wqb()
-        for s in range(0, UNITS + 2):
+        make_cosines()
+        transpose_x(2)
+        copy_x(2)
+        for s in range(1, UNITS + 2):
             step(s)

@@ -88,40 +88,33 @@ def tile_mlaattention_pa_t_kernel(tc, hidden_states, Wqa, Wqb, out):
         nc.vector.memset(warm[:], 0.0)
         nc.scalar.activation(out=warm[:, 1:2], in_=warm[:, 0:1], func=FUNC.Sin)
 
-        turns = const.tile([P, TILES_PER_BATCH, PAIRS, 2], F32)
-        for e, sign in enumerate((-1.0, 1.0)):
-            nc.vector.tensor_scalar_mul(out=turns[:, :, 0, e], in0=pos[:], scalar1=sign / (2.0 * math.pi))
+        turns = const.tile([P, TILES_PER_BATCH, PAIRS], F32)
+        nc.vector.tensor_scalar_mul(out=turns[:, :, 0], in0=pos[:], scalar1=1.0 / (2.0 * math.pi))
         known = 1
         while known < PAIRS:
             nc.vector.tensor_scalar_mul(
-                out=turns[:, :, known : 2 * known, :],
-                in0=turns[:, :, 0:known, :],
+                out=turns[:, :, known : 2 * known],
+                in0=turns[:, :, 0:known],
                 scalar1=ROPE_THETA ** (-2.0 * known / ROPE_DIM),
             )
             known *= 2
-        turns_flat = turns[:].rearrange("p t i e -> p (t i e)")
-        whole = const.tile([P, ANGLES * 2], I32)
+        turns_flat = turns[:].rearrange("p t i -> p (t i)")
+        whole = const.tile([P, ANGLES], I32)
         nc.vector.tensor_copy(out=whole[:], in_=turns_flat)
-        left = const.tile([P, ANGLES, 2], F32)
-        nc.vector.tensor_tensor(
-            out=left[:].rearrange("p a e -> p (a e)"), in0=turns_flat, in1=whole[:], op=ALU.subtract
-        )
+        left = const.tile([P, ANGLES], F32)
+        nc.vector.tensor_tensor(out=left[:], in0=turns_flat, in1=whole[:], op=ALU.subtract)
 
-        signed_sin = const.tile([P, ANGLES, 2], F32)
+        signed_sin = const.tile([P, 2, ANGLES], F32)
         half_sin = const.tile([P, ANGLES], F32)
         twice_sq = const.tile([P, ANGLES], F32)
         cos2 = const.tile([P, ANGLES, 2], F32)
 
         def make_sines():
-            nc.scalar.activation(
-                out=signed_sin[:].rearrange("p a e -> p (a e)"),
-                in_=left[:].rearrange("p a e -> p (a e)"),
-                func=FUNC.Sin,
-                scale=2.0 * math.pi,
-            )
+            for e, sign in enumerate((-1.0, 1.0)):
+                nc.scalar.activation(out=signed_sin[:, e], in_=left[:], func=FUNC.Sin, scale=sign * 2.0 * math.pi)
 
         def make_squares():
-            nc.scalar.activation(out=half_sin[:], in_=left[:, :, 1], func=FUNC.Sin, scale=math.pi)
+            nc.scalar.activation(out=half_sin[:], in_=left[:], func=FUNC.Sin, scale=math.pi)
             nc.scalar.activation(out=twice_sq[:], in_=half_sin[:], func=FUNC.Square, scale=math.sqrt(2.0))
 
         def make_cosines():
@@ -268,28 +261,29 @@ def tile_mlaattention_pa_t_kernel(tc, hidden_states, Wqa, Wqb, out):
             shape = [P, size, HEADS, PAIRS, 2]
             rotated = rope_banks[u][:, :size].rearrange("p i (h a e) -> p i h a e", h=HEADS, e=2)
             by_cos = rope_pool.tile([P, UNIT, HEADS, PAIRS, 2], F32)
-            by_sin = rope_pool.tile([P, UNIT, HEADS, PAIRS, 2], F32)
+            by_sin = rope_pool.tile([P, 2, UNIT, HEADS, PAIRS], F32)
             nc.vector.tensor_tensor(
                 out=by_cos[:, :size],
                 in0=rotated,
                 in1=cos2[:, here, :].rearrange("p (i a) e -> p i a e", i=size).unsqueeze(2).to_broadcast(shape),
                 op=ALU.mult,
             )
-            nc.vector.tensor_tensor(
-                out=by_sin[:, :size],
-                in0=rotated[:, :, :, :, ::-1],
-                in1=signed_sin[:, here, :].rearrange("p (i a) e -> p i a e", i=size).unsqueeze(2).to_broadcast(shape),
-                op=ALU.mult,
-            )
+            for e in range(2):
+                nc.vector.tensor_tensor(
+                    out=by_sin[:, e, :size],
+                    in0=rotated[:, :, :, :, 1 - e],
+                    in1=signed_sin[:, e, here].rearrange("p (i a) -> p i a", i=size).unsqueeze(2).to_broadcast(shape[:4]),
+                    op=ALU.mult,
+                )
             rope_tiles[u] = (by_cos, by_sin)
 
         def rope_sum(u):
             size = len(UNIT_TILES[u])
             by_cos, by_sin = rope_tiles[u]
             nc.vector.tensor_tensor(
-                out=out_tiles[u][:, :, :size, NOPE_DIM:HEAD_DIM].rearrange("p h i d -> p i h d"),
-                in0=by_cos[:, :size].rearrange("p i h a e -> p i h (a e)"),
-                in1=by_sin[:, :size].rearrange("p i h a e -> p i h (a e)"),
+                out=out_tiles[u][:, :, :size, NOPE_DIM:HEAD_DIM].rearrange("p h i (a e) -> p i h a e", e=2),
+                in0=by_cos[:, :size],
+                in1=by_sin[:, :, :size].rearrange("p e i h a -> p i h a e"),
                 op=ALU.add,
             )
 

@@ -32,6 +32,7 @@ UNIT = 2
 UNIT_TILES = [(n, n + 1) for n in range(0, N_TILES - UNIT, UNIT)] + [(N_TILES - 2,), (N_TILES - 1,)]
 UNITS = len(UNIT_TILES)
 ANGLES = TILES_PER_BATCH * PAIRS
+FIRST_RUN = 4
 LOADS = N_TILES // UNIT
 
 FLOPS = 2 * BATCH * SEQ * (D_MODEL * Q_LATENT + Q_LATENT * HEADS * HEAD_DIM)
@@ -47,7 +48,7 @@ def tile_mlaattention_pa_t_kernel(tc, hidden_states, Wqa, Wqb, out):
         xq_pool = ctx.enter_context(tc.tile_pool(name="xq", bufs=3))
         lat_pool = ctx.enter_context(tc.tile_pool(name="lat", bufs=3))
         rope_pool = ctx.enter_context(tc.tile_pool(name="rope", bufs=2))
-        out_pool = ctx.enter_context(tc.tile_pool(name="outp", bufs=4))
+        out_pool = ctx.enter_context(tc.tile_pool(name="outp", bufs=6))
         xt_psum = ctx.enter_context(tc.psum_pool(name="xt_psum", bufs=3))
         lat_psum = ctx.enter_context(tc.psum_pool(name="lat_psum", bufs=2))
         nope_psum = ctx.enter_context(tc.psum_pool(name="nope_psum", bufs=1))
@@ -89,43 +90,45 @@ def tile_mlaattention_pa_t_kernel(tc, hidden_states, Wqa, Wqb, out):
         nc.scalar.activation(out=warm[:, 1:2], in_=warm[:, 0:1], func=FUNC.Sin)
 
         turns = const.tile([P, TILES_PER_BATCH, PAIRS], F32)
-        nc.vector.tensor_scalar_mul(out=turns[:, :, 0], in0=pos[:], scalar1=1.0 / (2.0 * math.pi))
-        known = 1
-        while known < PAIRS:
+        for i in range(FIRST_RUN):
             nc.vector.tensor_scalar_mul(
-                out=turns[:, :, known : 2 * known],
-                in0=turns[:, :, 0:known],
-                scalar1=ROPE_THETA ** (-2.0 * known / ROPE_DIM),
+                out=turns[:, :, i], in0=pos[:], scalar1=ROPE_THETA ** (-2.0 * i / ROPE_DIM) / (2.0 * math.pi)
             )
-            known *= 2
+        for i in range(FIRST_RUN, PAIRS, FIRST_RUN):
+            nc.vector.tensor_scalar_mul(
+                out=turns[:, :, i : i + FIRST_RUN],
+                in0=turns[:, :, 0:FIRST_RUN],
+                scalar1=ROPE_THETA ** (-2.0 * i / ROPE_DIM),
+            )
         turns_flat = turns[:].rearrange("p t i -> p (t i)")
         whole = const.tile([P, ANGLES], I32)
         nc.vector.tensor_copy(out=whole[:], in_=turns_flat)
-        left = const.tile([P, ANGLES], F32)
-        nc.vector.tensor_tensor(out=left[:], in0=turns_flat, in1=whole[:], op=ALU.subtract)
-
-        signed_sin = const.tile([P, 2, ANGLES], F32)
+        left = const.tile([P, TILES_PER_BATCH, PAIRS], F32)
+        left_flat = left[:].rearrange("p t i -> p (t i)")
+        nc.vector.tensor_tensor(out=left_flat, in0=turns_flat, in1=whole[:], op=ALU.subtract)
         half_sin = const.tile([P, ANGLES], F32)
         twice_sq = const.tile([P, ANGLES], F32)
-        cos2 = const.tile([P, ANGLES, 2], F32)
-
-        def make_sines():
-            for e, sign in enumerate((-1.0, 1.0)):
-                nc.scalar.activation(out=signed_sin[:, e], in_=left[:], func=FUNC.Sin, scale=sign * 2.0 * math.pi)
-
-        def make_squares():
-            nc.scalar.activation(out=half_sin[:], in_=left[:], func=FUNC.Sin, scale=math.pi)
-            nc.scalar.activation(out=twice_sq[:], in_=half_sin[:], func=FUNC.Square, scale=math.sqrt(2.0))
+        cosines = const.tile([P, TILES_PER_BATCH, 2, PAIRS], F32)
+        nc.scalar.activation(out=half_sin[:], in_=left_flat, func=FUNC.Sin, scale=math.pi)
+        nc.scalar.activation(out=twice_sq[:], in_=half_sin[:], func=FUNC.Square, scale=math.sqrt(2.0))
+        signed_sin = const.tile([P, TILES_PER_BATCH, 2, PAIRS], F32)
 
         def make_cosines():
             nc.vector.tensor_scalar(
-                out=cos2[:],
-                in0=twice_sq[:].unsqueeze(2).to_broadcast([P, ANGLES, 2]),
+                out=cosines[:],
+                in0=twice_sq[:]
+                .rearrange("p (t i) -> p t i", t=TILES_PER_BATCH)
+                .unsqueeze(2)
+                .to_broadcast([P, TILES_PER_BATCH, 2, PAIRS]),
                 scalar1=-1.0,
                 scalar2=1.0,
                 op0=ALU.mult,
                 op1=ALU.add,
             )
+
+        def make_sines():
+            for e, sign in enumerate((-1.0, 1.0)):
+                nc.scalar.activation(out=signed_sin[:, :, e, :], in_=left[:], func=FUNC.Sin, scale=sign * 2.0 * math.pi)
 
         wa_grouped = const.tile([P, LATENT_BLOCKS, PASSES_A, P, PACK], BF16, align_bytes=64)
         wa_codes = const.tile([P, LATENT_BLOCKS, PASSES_A, P], U32, align_bytes=64)
@@ -144,59 +147,64 @@ def tile_mlaattention_pa_t_kernel(tc, hidden_states, Wqa, Wqb, out):
                 in_=wa_grouped[:, m0:m1].rearrange("p m c q t -> p (m c q t)"),
             )
 
-        wb_grouped = const.tile([P, 2, HEADS, NOPE_DIM, PACK], BF16, align_bytes=64)
+        wb_grouped = const.tile([P, 2, HALF_Q, PACK], BF16, align_bytes=64)
         wb_codes = const.tile([P, 2, HALF_Q], U32, align_bytes=64)
         wb_scales = const.tile([P, 2, HALF_Q], U8, align_bytes=64)
 
-        def group_wqb(s):
+        def group_wqb_kept():
             nc.vector.tensor_copy(
-                out=wb_grouped[:, s],
-                in_=wb_raw[:].rearrange("p j (h s d) -> p s h d j", h=HEADS, s=2)[:, s],
+                out=wb_grouped[:, 0].rearrange("p (h d) j -> p h d j", h=HEADS),
+                in_=wb_raw[:].rearrange("p j (h s d) -> p s h d j", h=HEADS, s=2)[:, 0],
+            )
+
+        def group_wqb_rotated(e):
+            nc.vector.tensor_copy(
+                out=wb_grouped[:, 1].rearrange("p (e h i) j -> p e h i j", e=2, h=HEADS)[:, e],
+                in_=wb_raw[:].rearrange("p j (h s i e) -> p s e h i j", h=HEADS, s=2, e=2)[:, 1, e],
             )
 
         def quantise_wqb():
             nc.vector.quantize_mx(
                 out=wb_codes[:].rearrange("p s n -> p (s n)").bitcast(FP8X4),
                 scales=wb_scales[:].rearrange("p s n -> p (s n)"),
-                in_=wb_grouped[:].rearrange("p s h d j -> p (s h d j)"),
+                in_=wb_grouped[:].rearrange("p s n j -> p (s n j)"),
             )
 
         xt_banks, xg_tiles, xq_tiles = {}, {}, {}
         lat_banks, lat_tiles, latq_tiles = {}, {}, {}
         nope_banks, rope_banks, rope_tiles, out_tiles = {}, {}, {}, {}
 
-        def transpose_x(u):
-            for i, n in enumerate(UNIT_TILES[u]):
-                words = x_tiles[n // UNIT][:, n % UNIT, :].bitcast(F32)
-                xt = xt_psum.tile([P, WORDS // P, P], F32)
+        def transpose_x(g):
+            for i in range(UNIT):
+                words = x_tiles[g][:, i, :].bitcast(F32)
+                xt = xt_psum.tile([P, WORDS // P, P], F32, tag="xt")
                 for w in range(WORDS // P):
                     first = 2 * P * (w // 2) + w % 2
                     nc.tensor.transpose(xt[:, w, :], words[:, first : 2 * P * (w // 2 + 1) : 2], ident[:])
-                xt_banks[u, i] = xt
+                xt_banks[g, i] = xt
 
-        def copy_x(u):
+        def copy_x(g):
             xg = xg_pool.tile([P, UNIT, PASSES_A, P, PACK], BF16, align_bytes=64)
-            for i in range(len(UNIT_TILES[u])):
+            for i in range(UNIT):
                 nc.scalar.copy(
                     out=xg[:, i].rearrange("p c r t -> p c (r t)").bitcast(F32).rearrange("p c (r v) -> p c r v", v=2),
-                    in_=xt_banks[u, i][:].rearrange("p (c v) r -> p c r v", v=2),
+                    in_=xt_banks[g, i][:].rearrange("p (c v) r -> p c r v", v=2),
                 )
-            xg_tiles[u] = xg
+            xg_tiles[g] = xg
 
-        def quantise_x(u):
-            size = len(UNIT_TILES[u])
+        def quantise_x(g):
             x_codes = xq_pool.tile([P, UNIT, PASSES_A, P], U32, align_bytes=64)
             x_scales = xq_pool.tile([P, UNIT, PASSES_A, P], U8, align_bytes=64)
             nc.vector.quantize_mx(
-                out=x_codes[:, :size].rearrange("p i c r -> p (i c r)").bitcast(FP8X4),
-                scales=x_scales[:, :size].rearrange("p i c r -> p (i c r)"),
-                in_=xg_tiles[u][:, :size].rearrange("p i c r t -> p (i c r t)"),
+                out=x_codes[:].rearrange("p i c r -> p (i c r)").bitcast(FP8X4),
+                scales=x_scales[:].rearrange("p i c r -> p (i c r)"),
+                in_=xg_tiles[g][:].rearrange("p i c r t -> p (i c r t)"),
             )
-            xq_tiles[u] = (x_codes, x_scales)
+            xq_tiles[g] = (x_codes, x_scales)
 
         def first_matmul(u):
-            x_codes, x_scales = xq_tiles[u]
-            for i in range(len(UNIT_TILES[u])):
+            for i, n in enumerate(UNIT_TILES[u]):
+                x_codes, x_scales = xq_tiles[n // UNIT]
                 lat_ps = lat_psum.tile([P, LATENT_BLOCKS, P], F32)
                 for m in range(LATENT_BLOCKS):
                     for c in range(PASSES_A):
@@ -204,8 +212,8 @@ def tile_mlaattention_pa_t_kernel(tc, hidden_states, Wqa, Wqb, out):
                             out=lat_ps[:, m, :],
                             lhsT=wa_codes[:, m, c, :].bitcast(FP8X4),
                             lhsT_scale=wa_scales[:, m, c, :],
-                            rhs=x_codes[:, i, c, :].bitcast(FP8X4),
-                            rhs_scale=x_scales[:, i, c, :],
+                            rhs=x_codes[:, n % UNIT, c, :].bitcast(FP8X4),
+                            rhs_scale=x_scales[:, n % UNIT, c, :],
                             start=(c == 0),
                             stop=(c == PASSES_A - 1),
                         )
@@ -230,8 +238,14 @@ def tile_mlaattention_pa_t_kernel(tc, hidden_states, Wqa, Wqb, out):
 
         def second_matmul(u):
             lat_codes, lat_scales = latq_tiles[u]
-            nope_ps = nope_psum.tile([P, UNIT, HALF_Q], F32)
-            rope_ps = rope_psum.tile([P, UNIT, HALF_Q], F32)
+            if u < UNITS - 2:
+                nope_ps = nope_psum.tile([P, UNIT, HALF_Q], F32)
+            else:
+                nope_ps = xt_psum.tile([P, UNIT, HALF_Q], F32, tag="xt")
+            if u < UNITS - 1:
+                rope_ps = rope_psum.tile([P, UNIT, HALF_Q], F32)
+            else:
+                rope_ps = xt_psum.tile([P, UNIT, HALF_Q], F32, tag="xt")
             for i in range(len(UNIT_TILES[u])):
                 for s, q_ps in enumerate((nope_ps, rope_ps)):
                     nc.tensor.matmul_mx(
@@ -257,24 +271,22 @@ def tile_mlaattention_pa_t_kernel(tc, hidden_states, Wqa, Wqb, out):
         def rope_products(u):
             size = len(UNIT_TILES[u])
             t0 = UNIT_TILES[u][0] % TILES_PER_BATCH
-            here = slice(t0 * PAIRS, (t0 + size) * PAIRS)
-            shape = [P, size, HEADS, PAIRS, 2]
-            rotated = rope_banks[u][:, :size].rearrange("p i (h a e) -> p i h a e", h=HEADS, e=2)
-            by_cos = rope_pool.tile([P, UNIT, HEADS, PAIRS, 2], F32)
+            shape = [P, size, 2, HEADS, PAIRS]
+            rotated = rope_banks[u][:, :size].rearrange("p i (e h a) -> p i e h a", e=2, h=HEADS)
+            by_cos = rope_pool.tile([P, 2, UNIT, HEADS, PAIRS], F32)
             by_sin = rope_pool.tile([P, 2, UNIT, HEADS, PAIRS], F32)
             nc.vector.tensor_tensor(
-                out=by_cos[:, :size],
+                out=by_cos[:, :, :size].rearrange("p e i h a -> p i e h a"),
                 in0=rotated,
-                in1=cos2[:, here, :].rearrange("p (i a) e -> p i a e", i=size).unsqueeze(2).to_broadcast(shape),
+                in1=cosines[:, t0 : t0 + size].unsqueeze(3).to_broadcast(shape),
                 op=ALU.mult,
             )
-            for e in range(2):
-                nc.vector.tensor_tensor(
-                    out=by_sin[:, e, :size],
-                    in0=rotated[:, :, :, :, 1 - e],
-                    in1=signed_sin[:, e, here].rearrange("p (i a) -> p i a", i=size).unsqueeze(2).to_broadcast(shape[:4]),
-                    op=ALU.mult,
-                )
+            nc.vector.tensor_tensor(
+                out=by_sin[:, :, :size].rearrange("p e i h a -> p i e h a"),
+                in0=rotated[:, :, ::-1],
+                in1=signed_sin[:, t0 : t0 + size].unsqueeze(3).to_broadcast(shape),
+                op=ALU.mult,
+            )
             rope_tiles[u] = (by_cos, by_sin)
 
         def rope_sum(u):
@@ -282,7 +294,7 @@ def tile_mlaattention_pa_t_kernel(tc, hidden_states, Wqa, Wqb, out):
             by_cos, by_sin = rope_tiles[u]
             nc.vector.tensor_tensor(
                 out=out_tiles[u][:, :, :size, NOPE_DIM:HEAD_DIM].rearrange("p h i (a e) -> p i h a e", e=2),
-                in0=by_cos[:, :size],
+                in0=by_cos[:, :, :size].rearrange("p e i h a -> p i h a e"),
                 in1=by_sin[:, :, :size].rearrange("p e i h a -> p i h a e"),
                 op=ALU.add,
             )
@@ -295,30 +307,19 @@ def tile_mlaattention_pa_t_kernel(tc, hidden_states, Wqa, Wqb, out):
                 in_=out_tiles[u][:, :, :size, :],
             )
 
-        def live(u):
-            return 0 <= u < UNITS
-
-        def matmuls(s):
-            if live(s):
-                first_matmul(s)
-                copy_latent(s)
-            if live(s - 1):
-                quantise_latent(s - 1)
-                second_matmul(s - 1)
-                copy_nope(s - 1)
-
         def step(s):
-            matmuls(s)
-            if live(s + 2):
+            first_matmul(s)
+            copy_latent(s)
+            quantise_latent(s - 1)
+            second_matmul(s - 1)
+            copy_nope(s - 1)
+            if s + 2 < LOADS:
                 transpose_x(s + 2)
                 copy_x(s + 2)
-            if live(s - 2):
-                rope_products(s - 2)
-            if live(s + 1):
-                quantise_x(s + 1)
-            if live(s - 2):
-                rope_sum(s - 2)
-                store(s - 2)
+            rope_products(s - 2)
+            quantise_x(s + 1)
+            rope_sum(s - 2)
+            store(s - 2)
 
         transpose_x(0)
         copy_x(0)
@@ -331,14 +332,47 @@ def tile_mlaattention_pa_t_kernel(tc, hidden_states, Wqa, Wqb, out):
         quantise_wqa(2, 4)
         transpose_x(1)
         copy_x(1)
-        group_wqb(0)
-        matmuls(0)
-        make_squares()
-        quantise_x(1)
-        group_wqb(1)
-        quantise_wqb()
+        group_wqb_kept()
+        first_matmul(0)
+        copy_latent(0)
         make_cosines()
+        quantise_x(1)
+        group_wqb_rotated(0)
+        group_wqb_rotated(1)
         transpose_x(2)
         copy_x(2)
-        for s in range(1, UNITS + 2):
+        quantise_latent(0)
+        quantise_wqb()
+        first_matmul(1)
+        copy_latent(1)
+        second_matmul(0)
+        copy_nope(0)
+        quantise_x(2)
+        transpose_x(3)
+        copy_x(3)
+
+        for s in range(2, LOADS - 1):
             step(s)
+
+        first_matmul(UNITS - 2)
+        copy_latent(UNITS - 2)
+        quantise_latent(UNITS - 3)
+        first_matmul(UNITS - 1)
+        second_matmul(UNITS - 3)
+        copy_latent(UNITS - 1)
+        copy_nope(UNITS - 3)
+        rope_products(UNITS - 4)
+        for u in (UNITS - 2, UNITS - 1):
+            quantise_latent(u)
+            second_matmul(u)
+            copy_nope(u)
+        rope_sum(UNITS - 4)
+        store(UNITS - 4)
+        rope_products(UNITS - 3)
+        rope_products(UNITS - 2)
+        rope_sum(UNITS - 3)
+        store(UNITS - 3)
+        rope_products(UNITS - 1)
+        for u in (UNITS - 2, UNITS - 1):
+            rope_sum(u)
+            store(u)

@@ -29,11 +29,9 @@ LATENT_BLOCKS = Q_LATENT // P
 TILES_PER_BATCH = SEQ // P
 N_TILES = BATCH * TILES_PER_BATCH
 UNIT = 2
-UNIT_TILES = [(n, n + 1) for n in range(0, N_TILES - UNIT, UNIT)] + [(N_TILES - 2,), (N_TILES - 1,)]
-UNITS = len(UNIT_TILES)
+UNITS = N_TILES // UNIT
 ANGLES = TILES_PER_BATCH * PAIRS
 FIRST_RUN = 4
-LOADS = N_TILES // UNIT
 
 FLOPS = 2 * BATCH * SEQ * (D_MODEL * Q_LATENT + Q_LATENT * HEADS * HEAD_DIM)
 
@@ -43,11 +41,11 @@ def tile_mlaattention_pa_t_kernel(tc, hidden_states, Wqa, Wqb, out):
     with ExitStack() as ctx:
         ctx.enter_context(tc.manual_schedule())
         const = ctx.enter_context(tc.tile_pool(name="const", bufs=1))
-        x_pool = ctx.enter_context(tc.tile_pool(name="x", bufs=LOADS))
-        xg_pool = ctx.enter_context(tc.tile_pool(name="xg", bufs=3))
-        xq_pool = ctx.enter_context(tc.tile_pool(name="xq", bufs=3))
-        lat_pool = ctx.enter_context(tc.tile_pool(name="lat", bufs=3))
-        rope_pool = ctx.enter_context(tc.tile_pool(name="rope", bufs=2))
+        x_pool = ctx.enter_context(tc.tile_pool(name="x", bufs=UNITS))
+        xg_pool = ctx.enter_context(tc.tile_pool(name="xg", bufs=5))
+        xq_pool = ctx.enter_context(tc.tile_pool(name="xq", bufs=5))
+        lat_pool = ctx.enter_context(tc.tile_pool(name="lat", bufs=5))
+        rope_pool = ctx.enter_context(tc.tile_pool(name="rope", bufs=3))
         out_pool = ctx.enter_context(tc.tile_pool(name="outp", bufs=6))
         xt_psum = ctx.enter_context(tc.psum_pool(name="xt_psum", bufs=3))
         lat_psum = ctx.enter_context(tc.psum_pool(name="lat_psum", bufs=2))
@@ -57,22 +55,28 @@ def tile_mlaattention_pa_t_kernel(tc, hidden_states, Wqa, Wqb, out):
         wa_raw = const.tile([P, PASSES_A, PACK, Q_LATENT], BF16)
         wb_raw = const.tile([P, PACK, Q_LATENT], BF16)
         x_tiles = []
-        for g in range(LOADS):
+
+        def load_x(g, first=0, end=UNIT):
             b, t0 = divmod(g * UNIT, TILES_PER_BATCH)
-            x_sb = x_pool.tile([P, UNIT, D_MODEL], BF16)
             nc.sync.dma_start(
-                out=x_sb[:],
-                in_=hidden_states[b].rearrange("(r t) k -> r t k", t=TILES_PER_BATCH)[:, t0 : t0 + UNIT, :],
+                out=x_tiles[g][:, first:end, :],
+                in_=hidden_states[b].rearrange("(r t) k -> r t k", t=TILES_PER_BATCH)[:, t0 + first : t0 + end, :],
             )
+
+        for g in range(UNITS):
+            x_sb = x_pool.tile([P, UNIT, D_MODEL], BF16)
             x_tiles.append(x_sb)
-            if g == 0:
-                for c in range(PASSES_A):
-                    nc.sync.dma_start(
-                        out=wa_raw[:, c],
-                        in_=Wqa[c * K_PASS : (c + 1) * K_PASS, :].rearrange("(p j) n -> p j n", j=PACK),
-                    )
-            if g == 1:
-                nc.sync.dma_start(out=wb_raw[:], in_=Wqb.rearrange("(p j) n -> p j n", j=PACK))
+        load_x(0, 0, 1)
+        for c in range(PASSES_A):
+            nc.sync.dma_start(
+                out=wa_raw[:, c],
+                in_=Wqa[c * K_PASS : (c + 1) * K_PASS, :].rearrange("(p j) n -> p j n", j=PACK),
+            )
+        load_x(0, 1, 2)
+        load_x(1)
+        nc.sync.dma_start(out=wb_raw[:], in_=Wqb.rearrange("(p j) n -> p j n", j=PACK))
+        for g in range(2, UNITS):
+            load_x(g)
 
         pos = const.tile([P, TILES_PER_BATCH], F32)
         nc.gpsimd.iota(
@@ -174,8 +178,8 @@ def tile_mlaattention_pa_t_kernel(tc, hidden_states, Wqa, Wqb, out):
         lat_banks, lat_tiles, latq_tiles = {}, {}, {}
         nope_banks, rope_banks, rope_tiles, out_tiles = {}, {}, {}, {}
 
-        def transpose_x(g):
-            for i in range(UNIT):
+        def transpose_x(g, tiles=range(UNIT)):
+            for i in tiles:
                 words = x_tiles[g][:, i, :].bitcast(F32)
                 xt = xt_psum.tile([P, WORDS // P, P], F32, tag="xt")
                 for w in range(WORDS // P):
@@ -183,28 +187,31 @@ def tile_mlaattention_pa_t_kernel(tc, hidden_states, Wqa, Wqb, out):
                     nc.tensor.transpose(xt[:, w, :], words[:, first : 2 * P * (w // 2 + 1) : 2], ident[:])
                 xt_banks[g, i] = xt
 
-        def copy_x(g):
-            xg = xg_pool.tile([P, UNIT, PASSES_A, P, PACK], BF16, align_bytes=64)
-            for i in range(UNIT):
+        def copy_x(g, tiles=range(UNIT)):
+            if g not in xg_tiles:
+                xg = xg_pool.tile([P, UNIT, PASSES_A, P, PACK], BF16, align_bytes=64)
+                xg_tiles[g] = xg
+            for i in tiles:
                 nc.scalar.copy(
-                    out=xg[:, i].rearrange("p c r t -> p c (r t)").bitcast(F32).rearrange("p c (r v) -> p c r v", v=2),
+                    out=xg_tiles[g][:, i].rearrange("p c r t -> p c (r t)").bitcast(F32).rearrange("p c (r v) -> p c r v", v=2),
                     in_=xt_banks[g, i][:].rearrange("p (c v) r -> p c r v", v=2),
                 )
-            xg_tiles[g] = xg
 
-        def quantise_x(g):
-            x_codes = xq_pool.tile([P, UNIT, PASSES_A, P], U32, align_bytes=64)
-            x_scales = xq_pool.tile([P, UNIT, PASSES_A, P], U8, align_bytes=64)
+        def quantise_x(g, first=0, end=UNIT):
+            if g not in xq_tiles:
+                x_codes = xq_pool.tile([P, UNIT, PASSES_A, P], U32, align_bytes=64)
+                x_scales = xq_pool.tile([P, UNIT, PASSES_A, P], U8, align_bytes=64)
+                xq_tiles[g] = (x_codes, x_scales)
+            x_codes, x_scales = xq_tiles[g]
             nc.vector.quantize_mx(
-                out=x_codes[:].rearrange("p i c r -> p (i c r)").bitcast(FP8X4),
-                scales=x_scales[:].rearrange("p i c r -> p (i c r)"),
-                in_=xg_tiles[g][:].rearrange("p i c r t -> p (i c r t)"),
+                out=x_codes[:, first:end].rearrange("p i c r -> p (i c r)").bitcast(FP8X4),
+                scales=x_scales[:, first:end].rearrange("p i c r -> p (i c r)"),
+                in_=xg_tiles[g][:, first:end].rearrange("p i c r t -> p (i c r t)"),
             )
-            xq_tiles[g] = (x_codes, x_scales)
 
         def first_matmul(u):
-            for i, n in enumerate(UNIT_TILES[u]):
-                x_codes, x_scales = xq_tiles[n // UNIT]
+            x_codes, x_scales = xq_tiles[u]
+            for i in range(UNIT):
                 lat_ps = lat_psum.tile([P, LATENT_BLOCKS, P], F32)
                 for m in range(LATENT_BLOCKS):
                     for c in range(PASSES_A):
@@ -212,8 +219,8 @@ def tile_mlaattention_pa_t_kernel(tc, hidden_states, Wqa, Wqb, out):
                             out=lat_ps[:, m, :],
                             lhsT=wa_codes[:, m, c, :].bitcast(FP8X4),
                             lhsT_scale=wa_scales[:, m, c, :],
-                            rhs=x_codes[:, n % UNIT, c, :].bitcast(FP8X4),
-                            rhs_scale=x_scales[:, n % UNIT, c, :],
+                            rhs=x_codes[:, i, c, :].bitcast(FP8X4),
+                            rhs_scale=x_scales[:, i, c, :],
                             start=(c == 0),
                             stop=(c == PASSES_A - 1),
                         )
@@ -221,32 +228,30 @@ def tile_mlaattention_pa_t_kernel(tc, hidden_states, Wqa, Wqb, out):
 
         def copy_latent(u):
             lat = lat_pool.tile([P, UNIT, P, PACK], BF16, align_bytes=64)
-            for i in range(len(UNIT_TILES[u])):
+            for i in range(UNIT):
                 nc.scalar.copy(out=lat[:, i], in_=lat_banks[u, i][:].rearrange("p m r -> p r m"))
             lat_tiles[u] = lat
 
-        def quantise_latent(u):
-            size = len(UNIT_TILES[u])
+        def quantise_latent(u, parts=1):
             lat_codes = lat_pool.tile([P, UNIT, P], U32, align_bytes=64)
             lat_scales = lat_pool.tile([P, UNIT, P], U8, align_bytes=64)
-            nc.vector.quantize_mx(
-                out=lat_codes[:, :size].rearrange("p i r -> p (i r)").bitcast(FP8X4),
-                scales=lat_scales[:, :size].rearrange("p i r -> p (i r)"),
-                in_=lat_tiles[u][:, :size].rearrange("p i r m -> p (i r m)"),
-            )
+            for i in range(0, UNIT, UNIT // parts):
+                tiles = slice(i, i + UNIT // parts)
+                nc.vector.quantize_mx(
+                    out=lat_codes[:, tiles].rearrange("p i r -> p (i r)").bitcast(FP8X4),
+                    scales=lat_scales[:, tiles].rearrange("p i r -> p (i r)"),
+                    in_=lat_tiles[u][:, tiles].rearrange("p i r m -> p (i r m)"),
+                )
             latq_tiles[u] = (lat_codes, lat_scales)
 
         def second_matmul(u):
             lat_codes, lat_scales = latq_tiles[u]
-            if u < UNITS - 2:
+            if u < UNITS - 1:
                 nope_ps = nope_psum.tile([P, UNIT, HALF_Q], F32)
             else:
                 nope_ps = xt_psum.tile([P, UNIT, HALF_Q], F32, tag="xt")
-            if u < UNITS - 1:
-                rope_ps = rope_psum.tile([P, UNIT, HALF_Q], F32)
-            else:
-                rope_ps = xt_psum.tile([P, UNIT, HALF_Q], F32, tag="xt")
-            for i in range(len(UNIT_TILES[u])):
+            rope_ps = rope_psum.tile([P, UNIT, HALF_Q], F32)
+            for i in range(UNIT):
                 for s, q_ps in enumerate((nope_ps, rope_ps)):
                     nc.tensor.matmul_mx(
                         out=q_ps[:, i, :],
@@ -260,51 +265,50 @@ def tile_mlaattention_pa_t_kernel(tc, hidden_states, Wqa, Wqb, out):
             nope_banks[u], rope_banks[u] = nope_ps, rope_ps
 
         def copy_nope(u):
-            size = len(UNIT_TILES[u])
             o_sb = out_pool.tile([P, HEADS, UNIT, HEAD_DIM], F32)
             nc.scalar.copy(
-                out=o_sb[:, :, :size, 0:NOPE_DIM].rearrange("p h i d -> p i h d"),
-                in_=nope_banks[u][:, :size].rearrange("p i (h d) -> p i h d", h=HEADS),
+                out=o_sb[:, :, :, 0:NOPE_DIM].rearrange("p h i d -> p i h d"),
+                in_=nope_banks[u][:].rearrange("p i (h d) -> p i h d", h=HEADS),
             )
             out_tiles[u] = o_sb
-
-        def rope_products(u):
-            size = len(UNIT_TILES[u])
-            t0 = UNIT_TILES[u][0] % TILES_PER_BATCH
-            shape = [P, size, 2, HEADS, PAIRS]
-            rotated = rope_banks[u][:, :size].rearrange("p i (e h a) -> p i e h a", e=2, h=HEADS)
             by_cos = rope_pool.tile([P, 2, UNIT, HEADS, PAIRS], F32)
             by_sin = rope_pool.tile([P, 2, UNIT, HEADS, PAIRS], F32)
-            nc.vector.tensor_tensor(
-                out=by_cos[:, :, :size].rearrange("p e i h a -> p i e h a"),
-                in0=rotated,
-                in1=cosines[:, t0 : t0 + size].unsqueeze(3).to_broadcast(shape),
-                op=ALU.mult,
-            )
-            nc.vector.tensor_tensor(
-                out=by_sin[:, :, :size].rearrange("p e i h a -> p i e h a"),
-                in0=rotated[:, :, ::-1],
-                in1=signed_sin[:, t0 : t0 + size].unsqueeze(3).to_broadcast(shape),
-                op=ALU.mult,
-            )
             rope_tiles[u] = (by_cos, by_sin)
 
-        def rope_sum(u):
-            size = len(UNIT_TILES[u])
+        all_heads = slice(0, HEADS)
+
+        def rope_products(u, heads=all_heads):
+            by_cos, by_sin = rope_tiles[u]
+            t0 = u * UNIT % TILES_PER_BATCH
+            shape = [P, UNIT, 2, heads.stop - heads.start, PAIRS]
+            rotated = rope_banks[u][:].rearrange("p i (e h a) -> p i e h a", e=2, h=HEADS)[:, :, :, heads]
+            nc.vector.tensor_tensor(
+                out=by_cos[:, :, :, heads].rearrange("p e i h a -> p i e h a"),
+                in0=rotated,
+                in1=cosines[:, t0 : t0 + UNIT].unsqueeze(3).to_broadcast(shape),
+                op=ALU.mult,
+            )
+            nc.vector.tensor_tensor(
+                out=by_sin[:, :, :, heads].rearrange("p e i h a -> p i e h a"),
+                in0=rotated[:, :, ::-1],
+                in1=signed_sin[:, t0 : t0 + UNIT].unsqueeze(3).to_broadcast(shape),
+                op=ALU.mult,
+            )
+
+        def rope_sum(u, heads=all_heads):
             by_cos, by_sin = rope_tiles[u]
             nc.vector.tensor_tensor(
-                out=out_tiles[u][:, :, :size, NOPE_DIM:HEAD_DIM].rearrange("p h i (a e) -> p i h a e", e=2),
-                in0=by_cos[:, :, :size].rearrange("p e i h a -> p i h a e"),
-                in1=by_sin[:, :, :size].rearrange("p e i h a -> p i h a e"),
+                out=out_tiles[u][:, heads, :, NOPE_DIM:HEAD_DIM].rearrange("p h i (a e) -> p i h a e", e=2),
+                in0=by_cos[:, :, :, heads].rearrange("p e i h a -> p i h a e"),
+                in1=by_sin[:, :, :, heads].rearrange("p e i h a -> p i h a e"),
                 op=ALU.add,
             )
 
-        def store(u):
-            size = len(UNIT_TILES[u])
-            b, t0 = divmod(UNIT_TILES[u][0], TILES_PER_BATCH)
+        def store(u, heads=all_heads):
+            b, t0 = divmod(u * UNIT, TILES_PER_BATCH)
             nc.sync.dma_start(
-                out=out[b].rearrange("h (r t) d -> r h t d", t=TILES_PER_BATCH)[:, :, t0 : t0 + size, :],
-                in_=out_tiles[u][:, :, :size, :],
+                out=out[b].rearrange("h (r t) d -> r h t d", t=TILES_PER_BATCH)[:, heads, t0 : t0 + UNIT, :],
+                in_=out_tiles[u][:, heads],
             )
 
         def step(s):
@@ -313,7 +317,7 @@ def tile_mlaattention_pa_t_kernel(tc, hidden_states, Wqa, Wqb, out):
             quantise_latent(s - 1)
             second_matmul(s - 1)
             copy_nope(s - 1)
-            if s + 2 < LOADS:
+            if s + 2 < UNITS:
                 transpose_x(s + 2)
                 copy_x(s + 2)
             rope_products(s - 2)
@@ -321,15 +325,18 @@ def tile_mlaattention_pa_t_kernel(tc, hidden_states, Wqa, Wqb, out):
             rope_sum(s - 2)
             store(s - 2)
 
-        transpose_x(0)
-        copy_x(0)
+        transpose_x(0, [0])
+        copy_x(0, [0])
         group_wqa(nc.vector.tensor_copy, 0, 0, 4)
         group_wqa(nc.scalar.copy, 1, 2, 4)
         group_wqa(nc.vector.tensor_copy, 1, 0, 2)
-        quantise_x(0)
+        transpose_x(0, [1])
+        copy_x(0, [1])
+        quantise_x(0, 0, 1)
         make_sines()
         quantise_wqa(0, 2)
         quantise_wqa(2, 4)
+        quantise_x(0, 1, 2)
         transpose_x(1)
         copy_x(1)
         group_wqb_kept()
@@ -351,28 +358,27 @@ def tile_mlaattention_pa_t_kernel(tc, hidden_states, Wqa, Wqb, out):
         transpose_x(3)
         copy_x(3)
 
-        for s in range(2, LOADS - 1):
+        for s in range(2, UNITS - 1):
             step(s)
 
-        first_matmul(UNITS - 2)
-        copy_latent(UNITS - 2)
-        quantise_latent(UNITS - 3)
-        first_matmul(UNITS - 1)
-        second_matmul(UNITS - 3)
-        copy_latent(UNITS - 1)
-        copy_nope(UNITS - 3)
-        rope_products(UNITS - 4)
-        for u in (UNITS - 2, UNITS - 1):
-            quantise_latent(u)
-            second_matmul(u)
-            copy_nope(u)
-        rope_sum(UNITS - 4)
-        store(UNITS - 4)
-        rope_products(UNITS - 3)
-        rope_products(UNITS - 2)
-        rope_sum(UNITS - 3)
-        store(UNITS - 3)
-        rope_products(UNITS - 1)
-        for u in (UNITS - 2, UNITS - 1):
-            rope_sum(u)
-            store(u)
+        last = UNITS - 1
+        first_matmul(last)
+        copy_latent(last)
+        quantise_latent(last - 1)
+        second_matmul(last - 1)
+        copy_nope(last - 1)
+        rope_products(last - 2)
+        quantise_latent(last, parts=UNIT)
+        second_matmul(last)
+        copy_nope(last)
+        rope_sum(last - 2)
+        store(last - 2)
+        rope_products(last - 1)
+        halves = (slice(0, HEADS // 2), slice(HEADS // 2, HEADS))
+        rope_products(last, halves[0])
+        rope_sum(last - 1)
+        store(last - 1)
+        rope_products(last, halves[1])
+        for heads in halves:
+            rope_sum(last, heads)
+            store(last, heads)

import math
from contextlib import ExitStack

import concourse.mybir as mybir
from concourse.masks import make_identity

F32 = mybir.dt.float32
BF16 = mybir.dt.bfloat16
I32 = mybir.dt.int32
U32 = mybir.dt.uint32
U8 = mybir.dt.uint8
FP8X4 = mybir.dt.float8_e4m3fn_x4
ALU = mybir.AluOpType
FUNC = mybir.ActivationFunctionType

P = 128
PACK = 4
BATCH, SEQ, D_MODEL, Q_LATENT = 2, 2048, 1024, 512
HEADS, HEAD_DIM, NOPE_DIM = 4, 128, 64
ROPE_DIM = HEAD_DIM - NOPE_DIM
PAIRS = ROPE_DIM // 2
HALF_Q = HEADS * NOPE_DIM
ROPE_THETA = 10000.0

K_PASS = P * PACK
PASSES_A = D_MODEL // K_PASS
WORDS = D_MODEL // 2
LATENT_BLOCKS = Q_LATENT // P
TILES_PER_BATCH = SEQ // P
N_TILES = BATCH * TILES_PER_BATCH
UNIT = 2
UNITS = N_TILES // UNIT
ANGLES = TILES_PER_BATCH * PAIRS
FIRST_RUN = 4

FLOPS = 2 * BATCH * SEQ * (D_MODEL * Q_LATENT + Q_LATENT * HEADS * HEAD_DIM)


def tile_mlaattention_pa_t_kernel(tc, hidden_states, Wqa, Wqb, out):
    nc = tc.nc
    with ExitStack() as ctx:
        ctx.enter_context(tc.manual_schedule())
        const = ctx.enter_context(tc.tile_pool(name="const", bufs=1))
        x_pool = ctx.enter_context(tc.tile_pool(name="x", bufs=UNITS))
        xg_pool = ctx.enter_context(tc.tile_pool(name="xg", bufs=5))
        xq_pool = ctx.enter_context(tc.tile_pool(name="xq", bufs=5))
        lat_pool = ctx.enter_context(tc.tile_pool(name="lat", bufs=5))
        rope_pool = ctx.enter_context(tc.tile_pool(name="rope", bufs=3))
        out_pool = ctx.enter_context(tc.tile_pool(name="outp", bufs=6))
        xt_psum = ctx.enter_context(tc.psum_pool(name="xt_psum", bufs=3))
        lat_psum = ctx.enter_context(tc.psum_pool(name="lat_psum", bufs=2))
        nope_psum = ctx.enter_context(tc.psum_pool(name="nope_psum", bufs=1))
        rope_psum = ctx.enter_context(tc.psum_pool(name="rope_psum", bufs=2))

        wa_raw = const.tile([P, PASSES_A, PACK, Q_LATENT], BF16)
        wb_raw = const.tile([P, PACK, Q_LATENT], BF16)
        x_tiles = []

        def load_x(g, first=0, end=UNIT):
            b, t0 = divmod(g * UNIT, TILES_PER_BATCH)
            nc.sync.dma_start(
                out=x_tiles[g][:, first:end, :],
                in_=hidden_states[b].rearrange("(r t) k -> r t k", t=TILES_PER_BATCH)[:, t0 + first : t0 + end, :],
            )

        for g in range(UNITS):
            x_sb = x_pool.tile([P, UNIT, D_MODEL], BF16)
            x_tiles.append(x_sb)
        load_x(0, 0, 1)
        for c in range(PASSES_A):
            nc.sync.dma_start(
                out=wa_raw[:, c],
                in_=Wqa[c * K_PASS : (c + 1) * K_PASS, :].rearrange("(p j) n -> p j n", j=PACK),
            )
        load_x(0, 1, 2)
        load_x(1)
        nc.sync.dma_start(out=wb_raw[:], in_=Wqb.rearrange("(p j) n -> p j n", j=PACK))
        for g in range(2, UNITS):
            load_x(g)

        pos = const.tile([P, TILES_PER_BATCH], F32)
        nc.gpsimd.iota(
            pos[:],
            pattern=[[1, TILES_PER_BATCH]],
            base=0,
            channel_multiplier=TILES_PER_BATCH,
            allow_small_or_imprecise_dtypes=True,
        )
        ident = const.tile([P, P], F32)
        make_identity(nc, ident[:])

        warm = const.tile([P, 2], F32)
        nc.vector.memset(warm[:], 0.0)
        nc.scalar.activation(out=warm[:, 1:2], in_=warm[:, 0:1], func=FUNC.Sin)

        turns = const.tile([P, TILES_PER_BATCH, PAIRS], F32)
        for i in range(FIRST_RUN):
            nc.vector.tensor_scalar_mul(
                out=turns[:, :, i], in0=pos[:], scalar1=ROPE_THETA ** (-2.0 * i / ROPE_DIM) / (2.0 * math.pi)
            )
        for i in range(FIRST_RUN, PAIRS, FIRST_RUN):
            nc.vector.tensor_scalar_mul(
                out=turns[:, :, i : i + FIRST_RUN],
                in0=turns[:, :, 0:FIRST_RUN],
                scalar1=ROPE_THETA ** (-2.0 * i / ROPE_DIM),
            )
        turns_flat = turns[:].rearrange("p t i -> p (t i)")
        whole = const.tile([P, ANGLES], I32)
        nc.vector.tensor_copy(out=whole[:], in_=turns_flat)
        left = const.tile([P, TILES_PER_BATCH, PAIRS], F32)
        left_flat = left[:].rearrange("p t i -> p (t i)")
        nc.vector.tensor_tensor(out=left_flat, in0=turns_flat, in1=whole[:], op=ALU.subtract)
        half_sin = const.tile([P, ANGLES], F32)
        twice_sq = const.tile([P, ANGLES], F32)
        cosines = const.tile([P, TILES_PER_BATCH, 2, PAIRS], F32)
        nc.scalar.activation(out=half_sin[:], in_=left_flat, func=FUNC.Sin, scale=math.pi)
        nc.scalar.activation(out=twice_sq[:], in_=half_sin[:], func=FUNC.Square, scale=math.sqrt(2.0))
        signed_sin = const.tile([P, TILES_PER_BATCH, 2, PAIRS], F32)

        def make_cosines():
            nc.vector.tensor_scalar(
                out=cosines[:],
                in0=twice_sq[:]
                .rearrange("p (t i) -> p t i", t=TILES_PER_BATCH)
                .unsqueeze(2)
                .to_broadcast([P, TILES_PER_BATCH, 2, PAIRS]),
                scalar1=-1.0,
                scalar2=1.0,
                op0=ALU.mult,
                op1=ALU.add,
            )

        def make_sines():
            for e, sign in enumerate((-1.0, 1.0)):
                nc.scalar.activation(out=signed_sin[:, :, e, :], in_=left[:], func=FUNC.Sin, scale=sign * 2.0 * math.pi)

        wa_grouped = const.tile([P, LATENT_BLOCKS, PASSES_A, P, PACK], BF16, align_bytes=64)
        wa_codes = const.tile([P, LATENT_BLOCKS, PASSES_A, P], U32, align_bytes=64)
        wa_scales = const.tile([P, LATENT_BLOCKS, PASSES_A, P], U8, align_bytes=64)

        def group_wqa(copy, c, m0, m1):
            copy(
                out=wa_grouped[:, m0:m1, c],
                in_=wa_raw[:, c].rearrange("p t (q m) -> p m q t", m=LATENT_BLOCKS)[:, m0:m1],
            )

        def quantise_wqa(m0, m1):
            nc.vector.quantize_mx(
                out=wa_codes[:, m0:m1].rearrange("p m c q -> p (m c q)").bitcast(FP8X4),
                scales=wa_scales[:, m0:m1].rearrange("p m c q -> p (m c q)"),
                in_=wa_grouped[:, m0:m1].rearrange("p m c q t -> p (m c q t)"),
            )

        wb_grouped = const.tile([P, 2, HALF_Q, PACK], BF16, align_bytes=64)
        wb_codes = const.tile([P, 2, HALF_Q], U32, align_bytes=64)
        wb_scales = const.tile([P, 2, HALF_Q], U8, align_bytes=64)

        def group_wqb_kept():
            nc.vector.tensor_copy(
                out=wb_grouped[:, 0].rearrange("p (h d) j -> p h d j", h=HEADS),
                in_=wb_raw[:].rearrange("p j (h s d) -> p s h d j", h=HEADS, s=2)[:, 0],
            )

        def group_wqb_rotated(e):
            nc.vector.tensor_copy(
                out=wb_grouped[:, 1].rearrange("p (e h i) j -> p e h i j", e=2, h=HEADS)[:, e],
                in_=wb_raw[:].rearrange("p j (h s i e) -> p s e h i j", h=HEADS, s=2, e=2)[:, 1, e],
            )

        def quantise_wqb():
            nc.vector.quantize_mx(
                out=wb_codes[:].rearrange("p s n -> p (s n)").bitcast(FP8X4),
                scales=wb_scales[:].rearrange("p s n -> p (s n)"),
                in_=wb_grouped[:].rearrange("p s n j -> p (s n j)"),
            )

        xt_banks, xg_tiles, xq_tiles = {}, {}, {}
        lat_banks, lat_tiles, latq_tiles = {}, {}, {}
        nope_banks, rope_banks, rope_tiles, out_tiles = {}, {}, {}, {}

        def transpose_x(g, tiles=range(UNIT)):
            for i in tiles:
                words = x_tiles[g][:, i, :].bitcast(F32)
                xt = xt_psum.tile([P, WORDS // P, P], F32, tag="xt")
                for w in range(WORDS // P):
                    first = 2 * P * (w // 2) + w % 2
                    nc.tensor.transpose(xt[:, w, :], words[:, first : 2 * P * (w // 2 + 1) : 2], ident[:])
                xt_banks[g, i] = xt

        def copy_x(g, tiles=range(UNIT)):
            if g not in xg_tiles:
                xg = xg_pool.tile([P, UNIT, PASSES_A, P, PACK], BF16, align_bytes=64)
                xg_tiles[g] = xg
            for i in tiles:
                nc.scalar.copy(
                    out=xg_tiles[g][:, i].rearrange("p c r t -> p c (r t)").bitcast(F32).rearrange("p c (r v) -> p c r v", v=2),
                    in_=xt_banks[g, i][:].rearrange("p (c v) r -> p c r v", v=2),
                )

        def quantise_x(g, first=0, end=UNIT):
            if g not in xq_tiles:
                x_codes = xq_pool.tile([P, UNIT, PASSES_A, P], U32, align_bytes=64)
                x_scales = xq_pool.tile([P, UNIT, PASSES_A, P], U8, align_bytes=64)
                xq_tiles[g] = (x_codes, x_scales)
            x_codes, x_scales = xq_tiles[g]
            nc.vector.quantize_mx(
                out=x_codes[:, first:end].rearrange("p i c r -> p (i c r)").bitcast(FP8X4),
                scales=x_scales[:, first:end].rearrange("p i c r -> p (i c r)"),
                in_=xg_tiles[g][:, first:end].rearrange("p i c r t -> p (i c r t)"),
            )

        def first_matmul(u):
            x_codes, x_scales = xq_tiles[u]
            for i in range(UNIT):
                lat_ps = lat_psum.tile([P, LATENT_BLOCKS, P], F32)
                for m in range(LATENT_BLOCKS):
                    for c in range(PASSES_A):
                        nc.tensor.matmul_mx(
                            out=lat_ps[:, m, :],
                            lhsT=wa_codes[:, m, c, :].bitcast(FP8X4),
                            lhsT_scale=wa_scales[:, m, c, :],
                            rhs=x_codes[:, i, c, :].bitcast(FP8X4),
                            rhs_scale=x_scales[:, i, c, :],
                            start=(c == 0),
                            stop=(c == PASSES_A - 1),
                        )
                lat_banks[u, i] = lat_ps

        def copy_latent(u):
            lat = lat_pool.tile([P, UNIT, P, PACK], BF16, align_bytes=64)
            for i in range(UNIT):
                nc.scalar.copy(out=lat[:, i], in_=lat_banks[u, i][:].rearrange("p m r -> p r m"))
            lat_tiles[u] = lat

        def quantise_latent(u, parts=1):
            lat_codes = lat_pool.tile([P, UNIT, P], U32, align_bytes=64)
            lat_scales = lat_pool.tile([P, UNIT, P], U8, align_bytes=64)
            for i in range(0, UNIT, UNIT // parts):
                tiles = slice(i, i + UNIT // parts)
                nc.vector.quantize_mx(
                    out=lat_codes[:, tiles].rearrange("p i r -> p (i r)").bitcast(FP8X4),
                    scales=lat_scales[:, tiles].rearrange("p i r -> p (i r)"),
                    in_=lat_tiles[u][:, tiles].rearrange("p i r m -> p (i r m)"),
                )
            latq_tiles[u] = (lat_codes, lat_scales)

        def second_matmul(u):
            lat_codes, lat_scales = latq_tiles[u]
            if u < UNITS - 1:
                nope_ps = nope_psum.tile([P, UNIT, HALF_Q], F32)
            else:
                nope_ps = xt_psum.tile([P, UNIT, HALF_Q], F32, tag="xt")
            rope_ps = rope_psum.tile([P, UNIT, HALF_Q], F32)
            for i in range(UNIT):
                for s, q_ps in enumerate((nope_ps, rope_ps)):
                    nc.tensor.matmul_mx(
                        out=q_ps[:, i, :],
                        lhsT=lat_codes[:, i, :].bitcast(FP8X4),
                        lhsT_scale=lat_scales[:, i, :],
                        rhs=wb_codes[:, s, :].bitcast(FP8X4),
                        rhs_scale=wb_scales[:, s, :],
                        start=True,
                        stop=True,
                    )
            nope_banks[u], rope_banks[u] = nope_ps, rope_ps

        def copy_nope(u):
            o_sb = out_pool.tile([P, HEADS, UNIT, HEAD_DIM], F32)
            nc.scalar.copy(
                out=o_sb[:, :, :, 0:NOPE_DIM].rearrange("p h i d -> p i h d"),
                in_=nope_banks[u][:].rearrange("p i (h d) -> p i h d", h=HEADS),
            )
            out_tiles[u] = o_sb
            by_cos = rope_pool.tile([P, 2, UNIT, HEADS, PAIRS], F32)
            by_sin = rope_pool.tile([P, 2, UNIT, HEADS, PAIRS], F32)
            rope_tiles[u] = (by_cos, by_sin)

        all_heads = slice(0, HEADS)

        def rope_products(u, heads=all_heads):
            by_cos, by_sin = rope_tiles[u]
            t0 = u * UNIT % TILES_PER_BATCH
            shape = [P, UNIT, 2, heads.stop - heads.start, PAIRS]
            rotated = rope_banks[u][:].rearrange("p i (e h a) -> p i e h a", e=2, h=HEADS)[:, :, :, heads]
            nc.vector.tensor_tensor(
                out=by_cos[:, :, :, heads].rearrange("p e i h a -> p i e h a"),
                in0=rotated,
                in1=cosines[:, t0 : t0 + UNIT].unsqueeze(3).to_broadcast(shape),
                op=ALU.mult,
            )
            nc.vector.tensor_tensor(
                out=by_sin[:, :, :, heads].rearrange("p e i h a -> p i e h a"),
                in0=rotated[:, :, ::-1],
                in1=signed_sin[:, t0 : t0 + UNIT].unsqueeze(3).to_broadcast(shape),
                op=ALU.mult,
            )

        def rope_sum(u, heads=all_heads):
            by_cos, by_sin = rope_tiles[u]
            nc.vector.tensor_tensor(
                out=out_tiles[u][:, heads, :, NOPE_DIM:HEAD_DIM].rearrange("p h i (a e) -> p i h a e", e=2),
                in0=by_cos[:, :, :, heads].rearrange("p e i h a -> p i h a e"),
                in1=by_sin[:, :, :, heads].rearrange("p e i h a -> p i h a e"),
                op=ALU.add,
            )

        def store(u, heads=all_heads):
            b, t0 = divmod(u * UNIT, TILES_PER_BATCH)
            nc.sync.dma_start(
                out=out[b].rearrange("h (r t) d -> r h t d", t=TILES_PER_BATCH)[:, heads, t0 : t0 + UNIT, :],
                in_=out_tiles[u][:, heads],
            )

        def step(s):
            first_matmul(s)
            copy_latent(s)
            quantise_latent(s - 1)
            second_matmul(s - 1)
            copy_nope(s - 1)
            if s + 2 < UNITS:
                transpose_x(s + 2)
                copy_x(s + 2)
            rope_products(s - 2)
            quantise_x(s + 1)
            rope_sum(s - 2)
            store(s - 2)

        transpose_x(0, [0])
        copy_x(0, [0])
        group_wqa(nc.vector.tensor_copy, 0, 0, 4)
        group_wqa(nc.scalar.copy, 1, 2, 4)
        group_wqa(nc.vector.tensor_copy, 1, 0, 2)
        transpose_x(0, [1])
        copy_x(0, [1])
        quantise_x(0, 0, 1)
        make_sines()
        quantise_wqa(0, 2)
        quantise_wqa(2, 4)
        quantise_x(0, 1, 2)
        transpose_x(1)
        copy_x(1)
        group_wqb_kept()
        first_matmul(0)
        copy_latent(0)
        make_cosines()
        quantise_x(1)
        group_wqb_rotated(0)
        group_wqb_rotated(1)
        transpose_x(2)
        copy_x(2)
        quantise_latent(0)
        quantise_wqb()
        first_matmul(1)
        copy_latent(1)
        second_matmul(0)
        copy_nope(0)
        quantise_x(2)
        transpose_x(3)
        copy_x(3)

        for s in range(2, UNITS - 1):
            step(s)

        last = UNITS - 1
        first_matmul(last)
        copy_latent(last)
        quantise_latent(last - 1)
        second_matmul(last - 1)
        copy_nope(last - 1)
        rope_products(last - 2)
        quantise_latent(last, parts=UNIT)
        second_matmul(last)
        copy_nope(last)
        rope_sum(last - 2)
        store(last - 2)
        rope_products(last - 1)
        halves = (slice(0, HEADS // 2), slice(HEADS // 2, HEADS))
        rope_products(last, halves[0])
        rope_sum(last - 1)
        store(last - 1)
        rope_products(last, halves[1])
        for heads in halves:
            rope_sum(last, heads)
            store(last, heads)
